import numpy as np
import ml_dtypes


def mxq(x, axis, fmt="e4m3"):
    dtype, down = {"e4m3": (ml_dtypes.float8_e4m3fn, 7), "e5m2": (ml_dtypes.float8_e5m2, 14)}[fmt]
    v = np.moveaxis(np.asarray(x, np.float32).astype(ml_dtypes.bfloat16).astype(np.float64), axis, -1)
    blocks = v.reshape(v.shape[:-1] + (-1, 32))
    amax = np.abs(blocks).max(-1, keepdims=True)
    byte = np.maximum(np.where(amax > 0, np.frexp(amax)[1] - 1 + 127, 0) - down, 1)
    scale = np.exp2(byte - 127.0)
    codes = (blocks / scale).astype(np.float32).astype(dtype).astype(np.float64)
    return np.moveaxis((codes * scale).reshape(v.shape), -1, axis)


WIDE = False


def mx_kscale(k):
    if not WIDE:
        return np.ones(k)
    levels = np.array([10, -10, 5, -5, 0])
    a = np.random.permutation(np.resize(levels, k // 512 * 4)).reshape(k // 512, 4)
    idx = np.arange(k)
    return np.exp2(a[idx // 512, idx % 128 // 32])


BF16 = ml_dtypes.bfloat16


def bf(x):
    return np.asarray(x, np.float32).astype(BF16)


def f64(x):
    return np.asarray(x).astype(np.float64)


B, C, S, OUT = 256, 4, 64, 128
IN = C * S * S
HS = S // 2
SUB, BLK = 4, 32


def haar_dwt2_features(x):
    x4 = x.reshape(x.shape[0], C, S, S)
    a = x4[:, :, 0::2, 0::2]
    bq = x4[:, :, 0::2, 1::2]
    c = x4[:, :, 1::2, 0::2]
    d = x4[:, :, 1::2, 1::2]
    LL = (a + bq + c + d) * 0.5
    LH = (a + bq - c - d) * 0.5
    HL = (a - bq + c - d) * 0.5
    HH = (a - bq - c + d) * 0.5
    t = np.stack([LL, LH, HL, HH], axis=2)
    return t.reshape(x.shape[0], -1)


def setup_inputs():
    g = mx_kscale(IN).reshape(-1, SUB, BLK)[:, 0, :].reshape(C, HS, HS)
    gx = np.repeat(np.repeat(g, 2, axis=1), 2, axis=2).reshape(IN)
    gt = np.repeat(g[:, None], SUB, axis=1).reshape(IN)
    return {"x": bf(np.random.standard_normal((B, IN)) * gx),
            "W": bf(np.random.standard_normal((OUT, IN)) * (1.0 / np.sqrt(IN)) / gt),
            "b": bf(np.random.standard_normal(OUT) * 0.5)}


def reference(x, W, b):
    t = haar_dwt2_features(f64(x))
    return (mxq(t, 1, "e4m3") @ mxq(f64(W), 1, "e4m3").T) + f64(b)

@@ -1,0 +1,138 @@
+from contextlib import ExitStack
+
+import concourse.mybir as mybir
+from concourse.masks import make_identity
+
+F32 = mybir.dt.float32
+BF16 = mybir.dt.bfloat16
+U32 = mybir.dt.uint32
+U8 = mybir.dt.uint8
+FP8X4 = mybir.dt.float8_e4m3fn_x4
+ADD = mybir.AluOpType.add
+SUB = mybir.AluOpType.subtract
+MULT = mybir.AluOpType.mult
+COPY = mybir.ActivationFunctionType.Copy
+
+P = 128
+B, C, S, OUT = 256, 4, 64, 128
+IN = C * S * S
+HS = S // 2
+H = B // P
+CHW = S * S
+NI = 4
+FLOPS = 2 * B * OUT * IN
+
+GPSIMD_UNITS = ()
+
+
+def tile_waveletlinearlayer_kernel(tc, x, W, b, out):
+    nc = tc.nc
+    with ExitStack() as ctx:
+        const = ctx.enter_context(tc.tile_pool(name="const", bufs=1))
+        xin = ctx.enter_context(tc.tile_pool(name="xin", bufs=6))
+        win = ctx.enter_context(tc.tile_pool(name="win", bufs=4))
+        sdp = ctx.enter_context(tc.tile_pool(name="sdp", bufs=3))
+        e1p = ctx.enter_context(tc.tile_pool(name="e1p", bufs=4))
+        grpp = ctx.enter_context(tc.tile_pool(name="grpp", bufs=3))
+        tqp = ctx.enter_context(tc.tile_pool(name="tqp", bufs=4))
+        wgp = ctx.enter_context(tc.tile_pool(name="wgp", bufs=2))
+        wqp = ctx.enter_context(tc.tile_pool(name="wqp", bufs=4))
+        accp = ctx.enter_context(tc.psum_pool(name="accp", bufs=1))
+        xtp = ctx.enter_context(tc.psum_pool(name="xtp", bufs=2))
+        wtp = ctx.enter_context(tc.psum_pool(name="wtp", bufs=2))
+
+        ident = const.tile([P, P], F32, name="ident")
+        make_identity(nc, ident[:])
+
+        x_sb = {}
+        w_sb = {}
+        for ch in range(C):
+            for h in range(H):
+                xt = xin.tile([P, CHW], BF16, name="xt")
+                nc.sync.dma_start(out=xt[:], in_=x[h * P:(h + 1) * P, ch * CHW:(ch + 1) * CHW])
+                x_sb[(h, ch)] = xt
+            wt = win.tile([P, CHW], BF16, name="wt")
+            nc.sync.dma_start(out=wt[:], in_=W[:, ch * CHW:(ch + 1) * CHW])
+            w_sb[ch] = wt
+        bias_sb = const.tile([P, OUT], BF16, name="bias_sb")
+        nc.sync.dma_start(out=bias_sb[:], in_=b.partition_broadcast(P))
+
+        acc0 = accp.tile([P, OUT], F32, name="acc0")
+        acc1 = accp.tile([P, OUT], F32, name="acc1")
+        acc = [acc0, acc1]
+
+        for ch in range(C):
+            sd = {}
+            for h in range(H):
+                sdt = sdp.tile([P, 2, 4, HS * 16], F32, name="sdt")
+                sd[h] = sdt
+                xv = x_sb[(h, ch)][:].rearrange("p (i r q v) -> p r v i q", i=HS, r=2, q=16, v=4)
+                for sigma in range(2):
+                    eng = nc.gpsimd if (h, sigma) in GPSIMD_UNITS else nc.vector
+                    eng.tensor_tensor(
+                        out=sdt[:, sigma].rearrange("p v (i q) -> p v i q", q=16),
+                        in0=xv[:, 0],
+                        in1=xv[:, 1],
+                        op=ADD if sigma == 0 else SUB,
+                    )
+
+            wv = w_sb[ch][:].bitcast(F32)
+            wg = wgp.tile([P, NI * 1024], BF16, name="wg", align_bytes=64)
+            wgv = wg[:].bitcast(F32).rearrange("p (g a o s) -> p g a o s", g=NI, a=2, o=OUT, s=2)
+            for g in range(NI):
+                wT = wtp.tile([P, 4, OUT], F32, name="wT")
+                for sub in range(4):
+                    c0 = sub * 512 + g * P
+                    nc.tensor.transpose(wT[:, sub, :], wv[:, c0:c0 + P], ident[:])
+                nc.scalar.copy(out=wgv[:, g], in_=wT[:].rearrange("p (a s) o -> p a o s", a=2, s=2))
+            wc = wqp.tile([P, NI * 256], U32, name="wc", align_bytes=64)
+            ws = wqp.tile([P, NI * 256], U8, name="ws", align_bytes=64)
+            nc.vector.quantize_mx(out=wc[:].bitcast(FP8X4), scales=ws[:], in_=wg[:])
+
+            for g in range(NI):
+                grp = grpp.tile([P, 2048], BF16, name="grp", align_bytes=64)
+                for h in range(H):
+                    e0 = xtp.tile([P, 4, P], F32, name="e0")
+                    e1 = xtp.tile([P, 4, P], F32, name="e1")
+                    ee = [e0, e1]
+                    for e in range(2):
+                        for sigma in range(2):
+                            for u in range(2):
+                                nc.tensor.transpose(
+                                    ee[e][:, 2 * sigma + u, :],
+                                    sd[h][:, sigma, 2 * u + e, g * P:(g + 1) * P],
+                                    ident[:],
+                                )
+                    e1s = e1p.tile([P, P, 4], F32, name="e1s")
+                    nc.scalar.activation(out=e1s[:], in_=e1[:].rearrange("p k n -> p n k"), func=COPY, scale=0.5)
+                    for a in range(2):
+                        c0 = (a * H + h) * 512
+                        nc.vector.scalar_tensor_tensor(
+                            out=grp[:, c0:c0 + 512].rearrange("p (n k) -> p n k", k=4),
+                            in0=e0[:].rearrange("p k n -> p n k"),
+                            scalar=0.5,
+                            in1=e1s[:],
+                            op0=MULT,
+                            op1=ADD if a == 0 else SUB,
+                        )
+                tcd = tqp.tile([P, 512], U32, name="tcd", align_bytes=64)
+                tsc = tqp.tile([P, 512], U8, name="tsc", align_bytes=64)
+                nc.vector.quantize_mx(out=tcd[:].bitcast(FP8X4), scales=tsc[:], in_=grp[:])
+                for a in range(2):
+                    for h in range(H):
+                        c0 = (a * H + h) * P
+                        w0 = (g * 2 + a) * OUT
+                        nc.tensor.matmul_mx(
+                            out=acc[h][:],
+                            lhsT=tcd[:, c0:c0 + P].bitcast(FP8X4),
+                            lhsT_scale=tsc[:, c0:c0 + P],
+                            rhs=wc[:, w0:w0 + OUT].bitcast(FP8X4),
+                            rhs_scale=ws[:, w0:w0 + OUT],
+                            start=(ch == 0 and g == 0 and a == 0),
+                            stop=(ch == C - 1 and g == NI - 1 and a == 1),
+                        )
+
+        for h in range(H):
+            res = const.tile([P, OUT], F32, name="res%d" % h)
+            nc.vector.tensor_tensor(out=res[:], in0=acc[h][:], in1=bias_sb[:], op=ADD)
+            nc.sync.dma_start(out=out[h * P:(h + 1) * P, :], in_=res[:])

@@ -22,7 +22,7 @@ CHW = S * S
 NI = 4
 FLOPS = 2 * B * OUT * IN
 
-GPSIMD_UNITS = ()
+NGP = 8
 
 
 def tile_waveletlinearlayer_kernel(tc, x, W, b, out):
@@ -31,29 +31,45 @@ def tile_waveletlinearlayer_kernel(tc, x, W, b, out):
         const = ctx.enter_context(tc.tile_pool(name="const", bufs=1))
         xin = ctx.enter_context(tc.tile_pool(name="xin", bufs=6))
         win = ctx.enter_context(tc.tile_pool(name="win", bufs=4))
-        sdp = ctx.enter_context(tc.tile_pool(name="sdp", bufs=3))
+        sdp = ctx.enter_context(tc.tile_pool(name="sdp", bufs=2))
         e1p = ctx.enter_context(tc.tile_pool(name="e1p", bufs=4))
-        grpp = ctx.enter_context(tc.tile_pool(name="grpp", bufs=3))
+        grpp = ctx.enter_context(tc.tile_pool(name="grpp", bufs=4))
         tqp = ctx.enter_context(tc.tile_pool(name="tqp", bufs=4))
         wgp = ctx.enter_context(tc.tile_pool(name="wgp", bufs=2))
         wqp = ctx.enter_context(tc.tile_pool(name="wqp", bufs=4))
         accp = ctx.enter_context(tc.psum_pool(name="accp", bufs=1))
         xtp = ctx.enter_context(tc.psum_pool(name="xtp", bufs=2))
         wtp = ctx.enter_context(tc.psum_pool(name="wtp", bufs=2))
+        ctx.enter_context(tc.manual_schedule())
 
         ident = const.tile([P, P], F32, name="ident")
         make_identity(nc, ident[:])
 
         x_sb = {}
         w_sb = {}
-        for ch in range(C):
-            for h in range(H):
-                xt = xin.tile([P, CHW], BF16, name="xt")
-                nc.sync.dma_start(out=xt[:], in_=x[h * P:(h + 1) * P, ch * CHW:(ch + 1) * CHW])
-                x_sb[(h, ch)] = xt
+
+        def load_x(h, ch, pieces):
+            xt = xin.tile([P, CHW], BF16, name="xt")
+            w = CHW // pieces
+            for k in range(pieces):
+                nc.sync.dma_start(
+                    out=xt[:, k * w:(k + 1) * w],
+                    in_=x[h * P:(h + 1) * P, ch * CHW + k * w:ch * CHW + (k + 1) * w],
+                )
+            x_sb[(h, ch)] = xt
+
+        def load_w(ch):
             wt = win.tile([P, CHW], BF16, name="wt")
             nc.sync.dma_start(out=wt[:], in_=W[:, ch * CHW:(ch + 1) * CHW])
             w_sb[ch] = wt
+
+        load_x(0, 0, 4)
+        load_x(1, 0, 1)
+        load_w(0)
+        for ch in range(1, C):
+            load_x(1, ch, 1)
+            load_x(0, ch, 1)
+            load_w(ch)
         bias_sb = const.tile([P, OUT], BF16, name="bias_sb")
         nc.sync.dma_start(out=bias_sb[:], in_=b.partition_broadcast(P))
 
@@ -61,76 +77,149 @@ def tile_waveletlinearlayer_kernel(tc, x, W, b, out):
         acc1 = accp.tile([P, OUT], F32, name="acc1")
         acc = [acc0, acc1]
 
-        for ch in range(C):
-            sd = {}
-            for h in range(H):
-                sdt = sdp.tile([P, 2, 4, HS * 16], F32, name="sdt")
-                sd[h] = sdt
-                xv = x_sb[(h, ch)][:].rearrange("p (i r q v) -> p r v i q", i=HS, r=2, q=16, v=4)
-                for sigma in range(2):
-                    eng = nc.gpsimd if (h, sigma) in GPSIMD_UNITS else nc.vector
-                    eng.tensor_tensor(
-                        out=sdt[:, sigma].rearrange("p v (i q) -> p v i q", q=16),
-                        in0=xv[:, 0],
-                        in1=xv[:, 1],
-                        op=ADD if sigma == 0 else SUB,
-                    )
+        sd = {}
+        wq = {}
+        grp = {}
+        tq = {}
+        ebank = {}
 
+        def new_sd(h, ch):
+            if h == 0:
+                sda = sdp.tile([P, 2, 4, HS * 16], F32, name="sda")
+                sd[(h, ch)] = sda
+            else:
+                sdb = sdp.tile([P, 2, 4, HS * 16], F32, name="sdb")
+                sd[(h, ch)] = sdb
+
+        def rows(eng, h, ch, sigma, g0, g1):
+            xv = x_sb[(h, ch)][:].rearrange("p (i r q v) -> p r v i q", i=HS, r=2, q=16, v=4)
+            eng.tensor_tensor(
+                out=sd[(h, ch)][:, sigma, :, g0 * P:g1 * P].rearrange("p v (i q) -> p v i q", q=16),
+                in0=xv[:, 0, :, 8 * g0:8 * g1, :],
+                in1=xv[:, 1, :, 8 * g0:8 * g1, :],
+                op=ADD if sigma == 0 else SUB,
+            )
+
+        def w_front(ch, g):
+            if g == 0:
+                wg = wgp.tile([P, NI * 1024], BF16, name="wg", align_bytes=64)
+                wq[("g", ch)] = wg
             wv = w_sb[ch][:].bitcast(F32)
-            wg = wgp.tile([P, NI * 1024], BF16, name="wg", align_bytes=64)
-            wgv = wg[:].bitcast(F32).rearrange("p (g a o s) -> p g a o s", g=NI, a=2, o=OUT, s=2)
-            for g in range(NI):
-                wT = wtp.tile([P, 4, OUT], F32, name="wT")
-                for sub in range(4):
-                    c0 = sub * 512 + g * P
-                    nc.tensor.transpose(wT[:, sub, :], wv[:, c0:c0 + P], ident[:])
-                nc.scalar.copy(out=wgv[:, g], in_=wT[:].rearrange("p (a s) o -> p a o s", a=2, s=2))
+            wgv = wq[("g", ch)][:].bitcast(F32).rearrange("p (g a o s) -> p g a o s", g=NI, a=2, o=OUT, s=2)
+            wT = wtp.tile([P, 4, OUT], F32, name="wT")
+            for sub in range(4):
+                c0 = sub * 512 + g * P
+                nc.tensor.transpose(wT[:, sub, :], wv[:, c0:c0 + P], ident[:])
+            nc.scalar.copy(out=wgv[:, g], in_=wT[:].rearrange("p (a s) o -> p a o s", a=2, s=2))
+
+        def w_quant(ch):
             wc = wqp.tile([P, NI * 256], U32, name="wc", align_bytes=64)
             ws = wqp.tile([P, NI * 256], U8, name="ws", align_bytes=64)
-            nc.vector.quantize_mx(out=wc[:].bitcast(FP8X4), scales=ws[:], in_=wg[:])
+            nc.vector.quantize_mx(out=wc[:].bitcast(FP8X4), scales=ws[:], in_=wq[("g", ch)][:])
+            wq[("c", ch)] = wc
+            wq[("s", ch)] = ws
 
-            for g in range(NI):
-                grp = grpp.tile([P, 2048], BF16, name="grp", align_bytes=64)
+        def front(ch, g, h):
+            e0 = xtp.tile([P, 4, P], F32, name="e0")
+            e1 = xtp.tile([P, 4, P], F32, name="e1")
+            ee = [e0, e1]
+            for e in (1, 0):
+                for sigma in range(2):
+                    for u in range(2):
+                        nc.tensor.transpose(
+                            ee[e][:, 2 * sigma + u, :],
+                            sd[(h, ch)][:, sigma, 2 * u + e, g * P:(g + 1) * P],
+                            ident[:],
+                        )
+            e1s = e1p.tile([P, P, 4], F32, name="e1s")
+            nc.scalar.activation(out=e1s[:], in_=e1[:].rearrange("p k n -> p n k"), func=COPY, scale=0.5)
+            ebank[(ch, g, h)] = (e0, e1s)
+
+        def back(ch, g, h):
+            if h == 0:
+                gt = grpp.tile([P, 2048], BF16, name="gt", align_bytes=64)
+                grp[(ch, g)] = gt
+            e0, e1s = ebank[(ch, g, h)]
+            for a in range(2):
+                c0 = (a * H + h) * 512
+                nc.vector.scalar_tensor_tensor(
+                    out=grp[(ch, g)][:, c0:c0 + 512].rearrange("p (n k) -> p n k", k=4),
+                    in0=e0[:].rearrange("p k n -> p n k"),
+                    scalar=0.5,
+                    in1=e1s[:],
+                    op0=MULT,
+                    op1=ADD if a == 0 else SUB,
+                )
+
+        def t_quant(ch, g):
+            tcd = tqp.tile([P, 512], U32, name="tcd", align_bytes=64)
+            tsc = tqp.tile([P, 512], U8, name="tsc", align_bytes=64)
+            nc.vector.quantize_mx(out=tcd[:].bitcast(FP8X4), scales=tsc[:], in_=grp[(ch, g)][:])
+            tq[(ch, g)] = (tcd, tsc)
+
+        def passes(ch, g):
+            tcd, tsc = tq[(ch, g)]
+            wc = wq[("c", ch)]
+            ws = wq[("s", ch)]
+            for a in range(2):
                 for h in range(H):
-                    e0 = xtp.tile([P, 4, P], F32, name="e0")
-                    e1 = xtp.tile([P, 4, P], F32, name="e1")
-                    ee = [e0, e1]
-                    for e in range(2):
-                        for sigma in range(2):
-                            for u in range(2):
-                                nc.tensor.transpose(
-                                    ee[e][:, 2 * sigma + u, :],
-                                    sd[h][:, sigma, 2 * u + e, g * P:(g + 1) * P],
-                                    ident[:],
-                                )
-                    e1s = e1p.tile([P, P, 4], F32, name="e1s")
-                    nc.scalar.activation(out=e1s[:], in_=e1[:].rearrange("p k n -> p n k"), func=COPY, scale=0.5)
-                    for a in range(2):
-                        c0 = (a * H + h) * 512
-                        nc.vector.scalar_tensor_tensor(
-                            out=grp[:, c0:c0 + 512].rearrange("p (n k) -> p n k", k=4),
-                            in0=e0[:].rearrange("p k n -> p n k"),
-                            scalar=0.5,
-                            in1=e1s[:],
-                            op0=MULT,
-                            op1=ADD if a == 0 else SUB,
-                        )
-                tcd = tqp.tile([P, 512], U32, name="tcd", align_bytes=64)
-                tsc = tqp.tile([P, 512], U8, name="tsc", align_bytes=64)
-                nc.vector.quantize_mx(out=tcd[:].bitcast(FP8X4), scales=tsc[:], in_=grp[:])
-                for a in range(2):
-                    for h in range(H):
-                        c0 = (a * H + h) * P
-                        w0 = (g * 2 + a) * OUT
-                        nc.tensor.matmul_mx(
-                            out=acc[h][:],
-                            lhsT=tcd[:, c0:c0 + P].bitcast(FP8X4),
-                            lhsT_scale=tsc[:, c0:c0 + P],
-                            rhs=wc[:, w0:w0 + OUT].bitcast(FP8X4),
-                            rhs_scale=ws[:, w0:w0 + OUT],
-                            start=(ch == 0 and g == 0 and a == 0),
-                            stop=(ch == C - 1 and g == NI - 1 and a == 1),
-                        )
+                    c0 = (a * H + h) * P
+                    w0 = (g * 2 + a) * OUT
+                    nc.tensor.matmul_mx(
+                        out=acc[h][:],
+                        lhsT=tcd[:, c0:c0 + P].bitcast(FP8X4),
+                        lhsT_scale=tsc[:, c0:c0 + P],
+                        rhs=wc[:, w0:w0 + OUT].bitcast(FP8X4),
+                        rhs_scale=ws[:, w0:w0 + OUT],
+                        start=(ch == 0 and g == 0 and a == 0),
+                        stop=(ch == C - 1 and g == NI - 1 and a == 1),
+                    )
+
+        new_sd(0, 0)
+        new_sd(1, 0)
+        for g0, g1 in ((0, 1), (1, 2), (2, 4)):
+            for sigma in range(2):
+                rows(nc.vector, 0, 0, sigma, g0, g1)
+        front(0, 0, 0)
+        for sigma in range(2):
+            rows(nc.vector, 1, 0, sigma, 0, NI)
+        for g in range(NI):
+            w_front(0, g)
+        front(0, 0, 1)
+
+        units = [(g, h) for g in range(NI) for h in range(H)]
+        for ch in range(C):
+            last = ch == C - 1
+            if not last:
+                new_sd(1, ch + 1)
+                for k in range(NGP):
+                    rows(nc.gpsimd, 1, ch + 1, k % 2, k // 2, k // 2 + 1)
+            for n in range(len(units)):
+                g, h = units[n]
+                back(ch, g, h)
+                if n + 2 < len(units):
+                    g2, h2 = units[n + 2]
+                    front(ch, g2, h2)
+                if h == 1 and not last:
+                    w_front(ch + 1, g)
+                if h == 1 and last:
+                    t_quant(ch, g)
+                    passes(ch, g)
+            if not last:
+                new_sd(0, ch + 1)
+                for sigma in range(2):
+                    rows(nc.vector, 0, ch + 1, sigma, 0, NI)
+                for k in range(NGP, 8):
+                    rows(nc.vector, 1, ch + 1, k % 2, k // 2, k // 2 + 1)
+                front(ch + 1, 0, 0)
+                front(ch + 1, 0, 1)
+                for g in range(NI):
+                    t_quant(ch, g)
+                if ch == 0:
+                    w_quant(0)
+                w_quant(ch + 1)
+                for g in range(NI):
+                    passes(ch, g)
 
         for h in range(H):
             res = const.tile([P, OUT], F32, name="res%d" % h)

@@ -22,54 +22,37 @@ CHW = S * S
 NI = 4
 FLOPS = 2 * B * OUT * IN
 
-NGP = 8
+NEG_ON_VECTOR = (0,)
 
 
 def tile_waveletlinearlayer_kernel(tc, x, W, b, out):
     nc = tc.nc
     with ExitStack() as ctx:
         const = ctx.enter_context(tc.tile_pool(name="const", bufs=1))
-        xin = ctx.enter_context(tc.tile_pool(name="xin", bufs=6))
-        win = ctx.enter_context(tc.tile_pool(name="win", bufs=4))
-        sdp = ctx.enter_context(tc.tile_pool(name="sdp", bufs=2))
-        e1p = ctx.enter_context(tc.tile_pool(name="e1p", bufs=4))
-        grpp = ctx.enter_context(tc.tile_pool(name="grpp", bufs=4))
+        xin = ctx.enter_context(tc.tile_pool(name="xin", bufs=4))
+        win = ctx.enter_context(tc.tile_pool(name="win", bufs=3))
+        sdp = ctx.enter_context(tc.tile_pool(name="sdp", bufs=4))
+        grpp = ctx.enter_context(tc.tile_pool(name="grpp", bufs=3))
         tqp = ctx.enter_context(tc.tile_pool(name="tqp", bufs=4))
         wgp = ctx.enter_context(tc.tile_pool(name="wgp", bufs=2))
         wqp = ctx.enter_context(tc.tile_pool(name="wqp", bufs=4))
         accp = ctx.enter_context(tc.psum_pool(name="accp", bufs=1))
         xtp = ctx.enter_context(tc.psum_pool(name="xtp", bufs=2))
         wtp = ctx.enter_context(tc.psum_pool(name="wtp", bufs=2))
-        ctx.enter_context(tc.manual_schedule())
 
         ident = const.tile([P, P], F32, name="ident")
         make_identity(nc, ident[:])
 
         x_sb = {}
         w_sb = {}
-
-        def load_x(h, ch, pieces):
-            xt = xin.tile([P, CHW], BF16, name="xt")
-            w = CHW // pieces
-            for k in range(pieces):
-                nc.sync.dma_start(
-                    out=xt[:, k * w:(k + 1) * w],
-                    in_=x[h * P:(h + 1) * P, ch * CHW + k * w:ch * CHW + (k + 1) * w],
-                )
-            x_sb[(h, ch)] = xt
-
-        def load_w(ch):
+        for ch in range(C):
+            for h in range(H):
+                xt = xin.tile([P, CHW], BF16, name="xt")
+                nc.sync.dma_start(out=xt[:], in_=x[h * P:(h + 1) * P, ch * CHW:(ch + 1) * CHW])
+                x_sb[(h, ch)] = xt
             wt = win.tile([P, CHW], BF16, name="wt")
             nc.sync.dma_start(out=wt[:], in_=W[:, ch * CHW:(ch + 1) * CHW])
             w_sb[ch] = wt
-
-        load_x(0, 0, 4)
-        load_x(1, 0, 1)
-        load_w(0)
-        for ch in range(1, C):
-            load_x(1, ch, 1)
-            load_x(0, ch, 1)
-            load_w(ch)
         bias_sb = const.tile([P, OUT], BF16, name="bias_sb")
         nc.sync.dma_start(out=bias_sb[:], in_=b.partition_broadcast(P))
 
@@ -77,149 +60,81 @@ def tile_waveletlinearlayer_kernel(tc, x, W, b, out):
         acc1 = accp.tile([P, OUT], F32, name="acc1")
         acc = [acc0, acc1]
 
-        sd = {}
-        wq = {}
-        grp = {}
-        tq = {}
-        ebank = {}
+        for ch in range(C):
+            sd = {}
+            nsd = {}
+            for h in range(H):
+                sdt = sdp.tile([P, 2, 4, HS * 16], F32, name="sdt")
+                sd[h] = sdt
+                xv = x_sb[(h, ch)][:].rearrange("p (i r q v) -> p r v i q", i=HS, r=2, q=16, v=4)
+                for sigma in range(2):
+                    nc.vector.tensor_tensor(
+                        out=sdt[:, sigma].rearrange("p v (i q) -> p v i q", q=16),
+                        in0=xv[:, 0],
+                        in1=xv[:, 1],
+                        op=ADD if sigma == 0 else SUB,
+                    )
+                nst = sdp.tile([P, 2, 2, HS * 16], F32, name="nst")
+                nsd[h] = nst
+                odd = sdt[:].rearrange("p s (u e) c -> p s u e c", e=2)[:, :, :, 1, :]
+                if h in NEG_ON_VECTOR:
+                    nc.vector.tensor_scalar_mul(out=nst[:], in0=odd, scalar1=-1.0)
+                else:
+                    nc.scalar.activation(out=nst[:], in_=odd, func=COPY, scale=-1.0)
 
-        def new_sd(h, ch):
-            if h == 0:
-                sda = sdp.tile([P, 2, 4, HS * 16], F32, name="sda")
-                sd[(h, ch)] = sda
-            else:
-                sdb = sdp.tile([P, 2, 4, HS * 16], F32, name="sdb")
-                sd[(h, ch)] = sdb
-
-        def rows(eng, h, ch, sigma, g0, g1):
-            xv = x_sb[(h, ch)][:].rearrange("p (i r q v) -> p r v i q", i=HS, r=2, q=16, v=4)
-            eng.tensor_tensor(
-                out=sd[(h, ch)][:, sigma, :, g0 * P:g1 * P].rearrange("p v (i q) -> p v i q", q=16),
-                in0=xv[:, 0, :, 8 * g0:8 * g1, :],
-                in1=xv[:, 1, :, 8 * g0:8 * g1, :],
-                op=ADD if sigma == 0 else SUB,
-            )
-
-        def w_front(ch, g):
-            if g == 0:
-                wg = wgp.tile([P, NI * 1024], BF16, name="wg", align_bytes=64)
-                wq[("g", ch)] = wg
             wv = w_sb[ch][:].bitcast(F32)
-            wgv = wq[("g", ch)][:].bitcast(F32).rearrange("p (g a o s) -> p g a o s", g=NI, a=2, o=OUT, s=2)
-            wT = wtp.tile([P, 4, OUT], F32, name="wT")
-            for sub in range(4):
-                c0 = sub * 512 + g * P
-                nc.tensor.transpose(wT[:, sub, :], wv[:, c0:c0 + P], ident[:])
-            nc.scalar.copy(out=wgv[:, g], in_=wT[:].rearrange("p (a s) o -> p a o s", a=2, s=2))
-
-        def w_quant(ch):
+            wg = wgp.tile([P, NI * 1024], BF16, name="wg", align_bytes=64)
+            wgv = wg[:].bitcast(F32).rearrange("p (g a o s) -> p g a o s", g=NI, a=2, o=OUT, s=2)
+            for g in range(NI):
+                wT = wtp.tile([P, 4, OUT], F32, name="wT")
+                for sub in range(4):
+                    c0 = sub * 512 + g * P
+                    nc.tensor.transpose(wT[:, sub, :], wv[:, c0:c0 + P], ident[:])
+                nc.scalar.copy(out=wgv[:, g], in_=wT[:].rearrange("p (a s) o -> p a o s", a=2, s=2))
             wc = wqp.tile([P, NI * 256], U32, name="wc", align_bytes=64)
             ws = wqp.tile([P, NI * 256], U8, name="ws", align_bytes=64)
-            nc.vector.quantize_mx(out=wc[:].bitcast(FP8X4), scales=ws[:], in_=wq[("g", ch)][:])
-            wq[("c", ch)] = wc
-            wq[("s", ch)] = ws
+            nc.vector.quantize_mx(out=wc[:].bitcast(FP8X4), scales=ws[:], in_=wg[:])
 
-        def front(ch, g, h):
-            e0 = xtp.tile([P, 4, P], F32, name="e0")
-            e1 = xtp.tile([P, 4, P], F32, name="e1")
-            ee = [e0, e1]
-            for e in (1, 0):
-                for sigma in range(2):
-                    for u in range(2):
-                        nc.tensor.transpose(
-                            ee[e][:, 2 * sigma + u, :],
-                            sd[(h, ch)][:, sigma, 2 * u + e, g * P:(g + 1) * P],
-                            ident[:],
-                        )
-            e1s = e1p.tile([P, P, 4], F32, name="e1s")
-            nc.scalar.activation(out=e1s[:], in_=e1[:].rearrange("p k n -> p n k"), func=COPY, scale=0.5)
-            ebank[(ch, g, h)] = (e0, e1s)
-
-        def back(ch, g, h):
-            if h == 0:
-                gt = grpp.tile([P, 2048], BF16, name="gt", align_bytes=64)
-                grp[(ch, g)] = gt
-            e0, e1s = ebank[(ch, g, h)]
-            for a in range(2):
-                c0 = (a * H + h) * 512
-                nc.vector.scalar_tensor_tensor(
-                    out=grp[(ch, g)][:, c0:c0 + 512].rearrange("p (n k) -> p n k", k=4),
-                    in0=e0[:].rearrange("p k n -> p n k"),
-                    scalar=0.5,
-                    in1=e1s[:],
-                    op0=MULT,
-                    op1=ADD if a == 0 else SUB,
-                )
-
-        def t_quant(ch, g):
-            tcd = tqp.tile([P, 512], U32, name="tcd", align_bytes=64)
-            tsc = tqp.tile([P, 512], U8, name="tsc", align_bytes=64)
-            nc.vector.quantize_mx(out=tcd[:].bitcast(FP8X4), scales=tsc[:], in_=grp[(ch, g)][:])
-            tq[(ch, g)] = (tcd, tsc)
-
-        def passes(ch, g):
-            tcd, tsc = tq[(ch, g)]
-            wc = wq[("c", ch)]
-            ws = wq[("s", ch)]
-            for a in range(2):
+            for g in range(NI):
+                grp = grpp.tile([P, 2048], BF16, name="grp", align_bytes=64)
+                cols = slice(g * P, (g + 1) * P)
                 for h in range(H):
-                    c0 = (a * H + h) * P
-                    w0 = (g * 2 + a) * OUT
-                    nc.tensor.matmul_mx(
-                        out=acc[h][:],
-                        lhsT=tcd[:, c0:c0 + P].bitcast(FP8X4),
-                        lhsT_scale=tsc[:, c0:c0 + P],
-                        rhs=wc[:, w0:w0 + OUT].bitcast(FP8X4),
-                        rhs_scale=ws[:, w0:w0 + OUT],
-                        start=(ch == 0 and g == 0 and a == 0),
-                        stop=(ch == C - 1 and g == NI - 1 and a == 1),
-                    )
-
-        new_sd(0, 0)
-        new_sd(1, 0)
-        for g0, g1 in ((0, 1), (1, 2), (2, 4)):
-            for sigma in range(2):
-                rows(nc.vector, 0, 0, sigma, g0, g1)
-        front(0, 0, 0)
-        for sigma in range(2):
-            rows(nc.vector, 1, 0, sigma, 0, NI)
-        for g in range(NI):
-            w_front(0, g)
-        front(0, 0, 1)
-
-        units = [(g, h) for g in range(NI) for h in range(H)]
-        for ch in range(C):
-            last = ch == C - 1
-            if not last:
-                new_sd(1, ch + 1)
-                for k in range(NGP):
-                    rows(nc.gpsimd, 1, ch + 1, k % 2, k // 2, k // 2 + 1)
-            for n in range(len(units)):
-                g, h = units[n]
-                back(ch, g, h)
-                if n + 2 < len(units):
-                    g2, h2 = units[n + 2]
-                    front(ch, g2, h2)
-                if h == 1 and not last:
-                    w_front(ch + 1, g)
-                if h == 1 and last:
-                    t_quant(ch, g)
-                    passes(ch, g)
-            if not last:
-                new_sd(0, ch + 1)
-                for sigma in range(2):
-                    rows(nc.vector, 0, ch + 1, sigma, 0, NI)
-                for k in range(NGP, 8):
-                    rows(nc.vector, 1, ch + 1, k % 2, k // 2, k // 2 + 1)
-                front(ch + 1, 0, 0)
-                front(ch + 1, 0, 1)
-                for g in range(NI):
-                    t_quant(ch, g)
-                if ch == 0:
-                    w_quant(0)
-                w_quant(ch + 1)
-                for g in range(NI):
-                    passes(ch, g)
+                    for a in range(2):
+                        bank = xtp.tile([P, 4, P], F32, name="bank%d" % a)
+                        for sigma in range(2):
+                            for u in range(2):
+                                second = sd[h][:, sigma, 2 * u + 1, cols] if a == 0 else nsd[h][:, sigma, u, cols]
+                                nc.tensor.matmul(
+                                    out=bank[:, 2 * sigma + u, :], lhsT=sd[h][:, sigma, 2 * u, cols], rhs=ident[:],
+                                    start=True, stop=False, is_transpose=True,
+                                )
+                                nc.tensor.matmul(
+                                    out=bank[:, 2 * sigma + u, :], lhsT=second, rhs=ident[:],
+                                    start=False, stop=True, is_transpose=True,
+                                )
+                        c0 = (a * H + h) * 512
+                        nc.scalar.activation(
+                            out=grp[:, c0:c0 + 512].rearrange("p (n k) -> p n k", k=4),
+                            in_=bank[:].rearrange("p k n -> p n k"),
+                            func=COPY,
+                            scale=0.5,
+                        )
+                tcd = tqp.tile([P, 512], U32, name="tcd", align_bytes=64)
+                tsc = tqp.tile([P, 512], U8, name="tsc", align_bytes=64)
+                nc.vector.quantize_mx(out=tcd[:].bitcast(FP8X4), scales=tsc[:], in_=grp[:])
+                for a in range(2):
+                    for h in range(H):
+                        c0 = (a * H + h) * P
+                        w0 = (g * 2 + a) * OUT
+                        nc.tensor.matmul_mx(
+                            out=acc[h][:],
+                            lhsT=tcd[:, c0:c0 + P].bitcast(FP8X4),
+                            lhsT_scale=tsc[:, c0:c0 + P],
+                            rhs=wc[:, w0:w0 + OUT].bitcast(FP8X4),
+                            rhs_scale=ws[:, w0:w0 + OUT],
+                            start=(ch == 0 and g == 0 and a == 0),
+                            stop=(ch == C - 1 and g == NI - 1 and a == 1),
+                        )
 
         for h in range(H):
             res = const.tile([P, OUT], F32, name="res%d" % h)

@@ -5,6 +5,7 @@ from concourse.masks import make_identity
 
 F32 = mybir.dt.float32
 BF16 = mybir.dt.bfloat16
+I32 = mybir.dt.int32
 U32 = mybir.dt.uint32
 U8 = mybir.dt.uint8
 FP8X4 = mybir.dt.float8_e4m3fn_x4
@@ -16,127 +17,231 @@ COPY = mybir.ActivationFunctionType.Copy
 P = 128
 B, C, S, OUT = 256, 4, 64, 128
 IN = C * S * S
-HS = S // 2
 H = B // P
 CHW = S * S
-NI = 4
+NBK = 8
+NHB = NBK * H
 FLOPS = 2 * B * OUT * IN
 
-NEG_ON_VECTOR = (0,)
+ZMAP = (1, 0, 1, 0, 1, 0, 1, 0, 1, 0, 1, 0, 1, 0, 0, 0)
+NW = 512
+LEAD = 3
+PAIR = 2
+NEG_VECTOR = 0
 
 
 def tile_waveletlinearlayer_kernel(tc, x, W, b, out):
     nc = tc.nc
+    PAD = NW - OUT
     with ExitStack() as ctx:
         const = ctx.enter_context(tc.tile_pool(name="const", bufs=1))
-        xin = ctx.enter_context(tc.tile_pool(name="xin", bufs=4))
+        xin = ctx.enter_context(tc.tile_pool(name="xin", bufs=6))
         win = ctx.enter_context(tc.tile_pool(name="win", bufs=3))
-        sdp = ctx.enter_context(tc.tile_pool(name="sdp", bufs=4))
-        grpp = ctx.enter_context(tc.tile_pool(name="grpp", bufs=3))
-        tqp = ctx.enter_context(tc.tile_pool(name="tqp", bufs=4))
+        sdp = ctx.enter_context(tc.tile_pool(name="sdp", bufs=LEAD + 2))
+        e1p = ctx.enter_context(tc.tile_pool(name="e1p", bufs=3))
+        grpp = ctx.enter_context(tc.tile_pool(name="grpp", bufs=2))
+        tqp = ctx.enter_context(tc.tile_pool(name="tqp", bufs=3))
         wgp = ctx.enter_context(tc.tile_pool(name="wgp", bufs=2))
-        wqp = ctx.enter_context(tc.tile_pool(name="wqp", bufs=4))
         accp = ctx.enter_context(tc.psum_pool(name="accp", bufs=1))
         xtp = ctx.enter_context(tc.psum_pool(name="xtp", bufs=2))
         wtp = ctx.enter_context(tc.psum_pool(name="wtp", bufs=2))
+        ctx.enter_context(tc.manual_schedule())
 
         ident = const.tile([P, P], F32, name="ident")
         make_identity(nc, ident[:])
 
+        wc = const.tile([P, PAD + 32 * OUT], U32, name="wc", align_bytes=64)
+        ws = const.tile([P, PAD + 32 * OUT], U8, name="ws", align_bytes=64)
+        if PAD:
+            nc.vector.memset(wc[:, 0:PAD].bitcast(I32), 0)
+            nc.vector.memset(ws[:, 0:PAD].bitcast(I32), 0)
+
         x_sb = {}
         w_sb = {}
-        for ch in range(C):
-            for h in range(H):
-                xt = xin.tile([P, CHW], BF16, name="xt")
-                nc.sync.dma_start(out=xt[:], in_=x[h * P:(h + 1) * P, ch * CHW:(ch + 1) * CHW])
-                x_sb[(h, ch)] = xt
+
+        def load_x(hb):
+            bk, h = hb // H, hb % H
+            xt = xin.tile([P, CHW // 2], BF16, name="xt")
+            c0 = bk * (CHW // 2)
+            nc.sync.dma_start(out=xt[:], in_=x[h * P:(h + 1) * P, c0:c0 + CHW // 2])
+            x_sb[hb] = xt
+
+        def load_w(ch):
             wt = win.tile([P, CHW], BF16, name="wt")
             nc.sync.dma_start(out=wt[:], in_=W[:, ch * CHW:(ch + 1) * CHW])
             w_sb[ch] = wt
+
+        load_x(0)
+        load_x(1)
+        load_x(2)
+        load_w(0)
+        load_x(3)
+        for ch in range(1, C):
+            load_x(4 * ch)
+            load_x(4 * ch + 1)
+            load_w(ch)
+            load_x(4 * ch + 2)
+            load_x(4 * ch + 3)
         bias_sb = const.tile([P, OUT], BF16, name="bias_sb")
         nc.sync.dma_start(out=bias_sb[:], in_=b.partition_broadcast(P))
 
-        acc0 = accp.tile([P, OUT], F32, name="acc0")
-        acc1 = accp.tile([P, OUT], F32, name="acc1")
+        acc0 = accp.tile([P, NW], F32, name="acc0")
+        acc1 = accp.tile([P, NW], F32, name="acc1")
         acc = [acc0, acc1]
 
-        for ch in range(C):
-            sd = {}
-            nsd = {}
-            for h in range(H):
-                sdt = sdp.tile([P, 2, 4, HS * 16], F32, name="sdt")
-                sd[h] = sdt
-                xv = x_sb[(h, ch)][:].rearrange("p (i r q v) -> p r v i q", i=HS, r=2, q=16, v=4)
-                for sigma in range(2):
-                    nc.vector.tensor_tensor(
-                        out=sdt[:, sigma].rearrange("p v (i q) -> p v i q", q=16),
-                        in0=xv[:, 0],
-                        in1=xv[:, 1],
-                        op=ADD if sigma == 0 else SUB,
-                    )
-                nst = sdp.tile([P, 2, 2, HS * 16], F32, name="nst")
-                nsd[h] = nst
-                odd = sdt[:].rearrange("p s (u e) c -> p s u e c", e=2)[:, :, :, 1, :]
-                if h in NEG_ON_VECTOR:
+        sd = {}
+        nsd = {}
+        grp = {}
+        tq = {}
+        wgt = {}
+        pending = []
+        cursor = [0]
+        ripe = [0]
+
+        def prep(hb):
+            sdt = sdp.tile([P, 2, 4, 256], F32, name="sdt")
+            sd[hb] = sdt
+            xv = x_sb[hb][:].rearrange("p (i r q v) -> p r v i q", i=16, r=2, q=16, v=4)
+            for sigma in range(2):
+                nc.vector.tensor_tensor(
+                    out=sdt[:, sigma].rearrange("p v (i q) -> p v i q", q=16),
+                    in0=xv[:, 0],
+                    in1=xv[:, 1],
+                    op=ADD if sigma == 0 else SUB,
+                )
+
+        def prep_neg(hb):
+            if ZMAP[hb]:
+                nst = sdp.tile([P, 2, 2, 256], F32, name="nst")
+                nsd[hb] = nst
+                odd = sd[hb][:].rearrange("p s (u e) c -> p s u e c", e=2)[:, :, :, 1, :]
+                if NEG_VECTOR:
                     nc.vector.tensor_scalar_mul(out=nst[:], in0=odd, scalar1=-1.0)
                 else:
                     nc.scalar.activation(out=nst[:], in_=odd, func=COPY, scale=-1.0)
 
+        def w_front(bk, gl):
+            ch, g = bk // 2, 2 * (bk % 2) + gl
+            if gl == 0:
+                wg = wgp.tile([P, 2048], BF16, name="wg", align_bytes=64)
+                wgt[bk] = wg
             wv = w_sb[ch][:].bitcast(F32)
-            wg = wgp.tile([P, NI * 1024], BF16, name="wg", align_bytes=64)
-            wgv = wg[:].bitcast(F32).rearrange("p (g a o s) -> p g a o s", g=NI, a=2, o=OUT, s=2)
-            for g in range(NI):
-                wT = wtp.tile([P, 4, OUT], F32, name="wT")
-                for sub in range(4):
-                    c0 = sub * 512 + g * P
-                    nc.tensor.transpose(wT[:, sub, :], wv[:, c0:c0 + P], ident[:])
-                nc.scalar.copy(out=wgv[:, g], in_=wT[:].rearrange("p (a s) o -> p a o s", a=2, s=2))
-            wc = wqp.tile([P, NI * 256], U32, name="wc", align_bytes=64)
-            ws = wqp.tile([P, NI * 256], U8, name="ws", align_bytes=64)
-            nc.vector.quantize_mx(out=wc[:].bitcast(FP8X4), scales=ws[:], in_=wg[:])
+            wgv = wgt[bk][:].bitcast(F32).rearrange("p (g a o s) -> p g a o s", g=2, a=2, o=OUT, s=2)
+            wT = wtp.tile([P, 4, OUT], F32, name="wT")
+            for sub in range(4):
+                c0 = sub * 512 + g * P
+                nc.tensor.transpose(wT[:, sub, :], wv[:, c0:c0 + P], ident[:])
+            nc.scalar.copy(out=wgv[:, gl], in_=wT[:].rearrange("p (a s) o -> p a o s", a=2, s=2))
 
-            for g in range(NI):
-                grp = grpp.tile([P, 2048], BF16, name="grp", align_bytes=64)
-                cols = slice(g * P, (g + 1) * P)
-                for h in range(H):
-                    for a in range(2):
-                        bank = xtp.tile([P, 4, P], F32, name="bank%d" % a)
-                        for sigma in range(2):
-                            for u in range(2):
-                                second = sd[h][:, sigma, 2 * u + 1, cols] if a == 0 else nsd[h][:, sigma, u, cols]
-                                nc.tensor.matmul(
-                                    out=bank[:, 2 * sigma + u, :], lhsT=sd[h][:, sigma, 2 * u, cols], rhs=ident[:],
-                                    start=True, stop=False, is_transpose=True,
-                                )
-                                nc.tensor.matmul(
-                                    out=bank[:, 2 * sigma + u, :], lhsT=second, rhs=ident[:],
-                                    start=False, stop=True, is_transpose=True,
-                                )
-                        c0 = (a * H + h) * 512
-                        nc.scalar.activation(
-                            out=grp[:, c0:c0 + 512].rearrange("p (n k) -> p n k", k=4),
-                            in_=bank[:].rearrange("p k n -> p n k"),
-                            func=COPY,
-                            scale=0.5,
-                        )
-                tcd = tqp.tile([P, 512], U32, name="tcd", align_bytes=64)
-                tsc = tqp.tile([P, 512], U8, name="tsc", align_bytes=64)
-                nc.vector.quantize_mx(out=tcd[:].bitcast(FP8X4), scales=tsc[:], in_=grp[:])
+        def w_quant(bk):
+            c0 = PAD + bk * 512
+            nc.vector.quantize_mx(out=wc[:, c0:c0 + 512].bitcast(FP8X4), scales=ws[:, c0:c0 + 512], in_=wgt[bk][:])
+
+        def gslice(bk, gl, a, h):
+            c0 = ((gl * 2 + a) * H + h) * 512
+            return grp[bk][:, c0:c0 + 512].rearrange("p (n k) -> p n k", k=4)
+
+        def unit(hb, gl):
+            bk, h = hb // H, hb % H
+            if h == 0 and gl == 0:
+                gt = grpp.tile([P, 4096], BF16, name="gt", align_bytes=64)
+                grp[bk] = gt
+            cols = slice(gl * P, (gl + 1) * P)
+            pa = xtp.tile([P, 4, P], F32, name="pa")
+            pb = xtp.tile([P, 4, P], F32, name="pb")
+            s = sd[hb]
+            if ZMAP[hb]:
+                for a in range(2):
+                    bank = pa if a == 0 else pb
+                    for sigma in range(2):
+                        for u in range(2):
+                            second = s[:, sigma, 2 * u + 1, cols] if a == 0 else nsd[hb][:, sigma, u, cols]
+                            nc.tensor.matmul(
+                                out=bank[:, 2 * sigma + u, :], lhsT=s[:, sigma, 2 * u, cols], rhs=ident[:],
+                                start=True, stop=False, is_transpose=True,
+                            )
+                            nc.tensor.matmul(
+                                out=bank[:, 2 * sigma + u, :], lhsT=second, rhs=ident[:],
+                                start=False, stop=True, is_transpose=True,
+                            )
+                    nc.scalar.activation(
+                        out=gslice(bk, gl, a, h), in_=bank[:].rearrange("p k n -> p n k"), func=COPY, scale=0.5,
+                    )
+                return None
+            for e in (1, 0):
+                bank = pa if e == 0 else pb
+                for sigma in range(2):
+                    for u in range(2):
+                        nc.tensor.transpose(bank[:, 2 * sigma + u, :], s[:, sigma, 2 * u + e, cols], ident[:])
+            e1s = e1p.tile([P, P, 4], F32, name="e1s")
+            nc.scalar.activation(out=e1s[:], in_=pb[:].rearrange("p k n -> p n k"), func=COPY, scale=0.5)
+            return (pa, e1s)
+
+        def combine(hb, gl, banks):
+            bk, h = hb // H, hb % H
+            pa, e1s = banks
+            for a in range(2):
+                nc.vector.scalar_tensor_tensor(
+                    out=gslice(bk, gl, a, h),
+                    in0=pa[:].rearrange("p k n -> p n k"),
+                    scalar=0.5,
+                    in1=e1s[:],
+                    op0=MULT,
+                    op1=ADD if a == 0 else SUB,
+                )
+
+        def t_quant(bk):
+            tcd = tqp.tile([P, 1024], U32, name="tcd", align_bytes=64)
+            tsc = tqp.tile([P, 1024], U8, name="tsc", align_bytes=64)
+            nc.vector.quantize_mx(out=tcd[:].bitcast(FP8X4), scales=tsc[:], in_=grp[bk][:])
+            tq[bk] = (tcd, tsc)
+            for gl in range(2):
                 for a in range(2):
                     for h in range(H):
-                        c0 = (a * H + h) * P
-                        w0 = (g * 2 + a) * OUT
-                        nc.tensor.matmul_mx(
-                            out=acc[h][:],
-                            lhsT=tcd[:, c0:c0 + P].bitcast(FP8X4),
-                            lhsT_scale=tsc[:, c0:c0 + P],
-                            rhs=wc[:, w0:w0 + OUT].bitcast(FP8X4),
-                            rhs_scale=ws[:, w0:w0 + OUT],
-                            start=(ch == 0 and g == 0 and a == 0),
-                            stop=(ch == C - 1 and g == NI - 1 and a == 1),
-                        )
+                        pending.append((bk, gl, a, h))
+
+        def passes(count):
+            for k in range(min(count, ripe[0] - cursor[0])):
+                bk, gl, a, h = pending[cursor[0]]
+                cursor[0] = cursor[0] + 1
+                tcd, tsc = tq[bk]
+                c0 = ((gl * 2 + a) * H + h) * P
+                w0 = (bk * 4 + gl * 2 + a) * OUT
+                nc.tensor.matmul_mx(
+                    out=acc[h][:],
+                    lhsT=tcd[:, c0:c0 + P].bitcast(FP8X4),
+                    lhsT_scale=tsc[:, c0:c0 + P],
+                    rhs=wc[:, w0:w0 + NW].bitcast(FP8X4),
+                    rhs_scale=ws[:, w0:w0 + NW],
+                    start=(bk == 0 and gl == 0 and a == 0),
+                    stop=(bk == NBK - 1 and gl == 1 and a == 1),
+                )
+
+        for hb in range(LEAD):
+            prep(hb)
+            prep_neg(hb)
+        for hb in range(NHB):
+            bk, h = hb // H, hb % H
+            ripe[0] = len(pending)
+            if hb + LEAD < NHB:
+                prep(hb + LEAD)
+            if h == 0 and bk > 0:
+                w_quant(bk - 1)
+                t_quant(bk - 1)
+            for gl in range(2):
+                banks = unit(hb, gl)
+                passes(PAIR)
+                if banks is not None:
+                    combine(hb, gl, banks)
+            w_front(bk, h)
+            if hb + LEAD < NHB:
+                prep_neg(hb + LEAD)
+        w_quant(NBK - 1)
+        t_quant(NBK - 1)
+        ripe[0] = len(pending)
+        passes(64)
 
         for h in range(H):
             res = const.tile([P, OUT], F32, name="res%d" % h)
-            nc.vector.tensor_tensor(out=res[:], in0=acc[h][:], in1=bias_sb[:], op=ADD)
+            nc.vector.tensor_tensor(out=res[:], in0=acc[h][:, PAD:PAD + OUT], in1=bias_sb[:], op=ADD)
             nc.sync.dma_start(out=out[h * P:(h + 1) * P, :], in_=res[:])

@@ -23,11 +23,16 @@ NBK = 8
 NHB = NBK * H
 FLOPS = 2 * B * OUT * IN
 
-ZMAP = (1, 0, 1, 0, 1, 0, 1, 0, 1, 0, 1, 0, 1, 0, 0, 0)
+ZMAP = (1, 0, 1, 0, 1, 0, 1, 0, 1, 0, 1, 0, 1, 0, 0, 1)
 NW = 512
 LEAD = 3
 PAIR = 2
 NEG_VECTOR = 0
+EB = 2
+RL = 2
+NL = 2
+FILL = 1
+WIDE = 2
 
 
 def tile_waveletlinearlayer_kernel(tc, x, W, b, out):
@@ -38,7 +43,7 @@ def tile_waveletlinearlayer_kernel(tc, x, W, b, out):
         xin = ctx.enter_context(tc.tile_pool(name="xin", bufs=6))
         win = ctx.enter_context(tc.tile_pool(name="win", bufs=3))
         sdp = ctx.enter_context(tc.tile_pool(name="sdp", bufs=LEAD + 2))
-        e1p = ctx.enter_context(tc.tile_pool(name="e1p", bufs=3))
+        e1p = ctx.enter_context(tc.tile_pool(name="e1p", bufs=EB))
         grpp = ctx.enter_context(tc.tile_pool(name="grpp", bufs=2))
         tqp = ctx.enter_context(tc.tile_pool(name="tqp", bufs=3))
         wgp = ctx.enter_context(tc.tile_pool(name="wgp", bufs=2))
@@ -55,15 +60,23 @@ def tile_waveletlinearlayer_kernel(tc, x, W, b, out):
         if PAD:
             nc.vector.memset(wc[:, 0:PAD].bitcast(I32), 0)
             nc.vector.memset(ws[:, 0:PAD].bitcast(I32), 0)
+        zc = const.tile([P, NW], U32, name="zc", align_bytes=64)
+        zs = const.tile([P, NW], U8, name="zs", align_bytes=64)
+        if FILL:
+            zb = const.tile([P, 4 * NW], BF16, name="zb", align_bytes=64)
+            nc.vector.memset(zb[:].bitcast(I32), 0)
+            nc.vector.quantize_mx(out=zc[:].bitcast(FP8X4), scales=zs[:], in_=zb[:])
 
         x_sb = {}
         w_sb = {}
 
-        def load_x(hb):
+        def load_x(hb, parts):
             bk, h = hb // H, hb % H
             xt = xin.tile([P, CHW // 2], BF16, name="xt")
-            c0 = bk * (CHW // 2)
-            nc.sync.dma_start(out=xt[:], in_=x[h * P:(h + 1) * P, c0:c0 + CHW // 2])
+            w = CHW // 2 // parts
+            for k in range(parts):
+                c0 = bk * (CHW // 2) + k * w
+                nc.sync.dma_start(out=xt[:, k * w:(k + 1) * w], in_=x[h * P:(h + 1) * P, c0:c0 + w])
             x_sb[hb] = xt
 
         def load_w(ch):
@@ -71,17 +84,17 @@ def tile_waveletlinearlayer_kernel(tc, x, W, b, out):
             nc.sync.dma_start(out=wt[:], in_=W[:, ch * CHW:(ch + 1) * CHW])
             w_sb[ch] = wt
 
-        load_x(0)
-        load_x(1)
-        load_x(2)
+        load_x(0, 2)
+        load_x(1, 1)
+        load_x(2, 1)
         load_w(0)
-        load_x(3)
+        load_x(3, 1)
         for ch in range(1, C):
-            load_x(4 * ch)
-            load_x(4 * ch + 1)
+            load_x(4 * ch, 1)
+            load_x(4 * ch + 1, 1)
             load_w(ch)
-            load_x(4 * ch + 2)
-            load_x(4 * ch + 3)
+            load_x(4 * ch + 2, 1)
+            load_x(4 * ch + 3, 1)
         bias_sb = const.tile([P, OUT], BF16, name="bias_sb")
         nc.sync.dma_start(out=bias_sb[:], in_=b.partition_broadcast(P))
 
@@ -94,21 +107,25 @@ def tile_waveletlinearlayer_kernel(tc, x, W, b, out):
         grp = {}
         tq = {}
         wgt = {}
+        halves = {}
         pending = []
         cursor = [0]
         ripe = [0]
+        hist = []
 
-        def prep(hb):
+        def prep(hb, parts):
             sdt = sdp.tile([P, 2, 4, 256], F32, name="sdt")
             sd[hb] = sdt
             xv = x_sb[hb][:].rearrange("p (i r q v) -> p r v i q", i=16, r=2, q=16, v=4)
-            for sigma in range(2):
-                nc.vector.tensor_tensor(
-                    out=sdt[:, sigma].rearrange("p v (i q) -> p v i q", q=16),
-                    in0=xv[:, 0],
-                    in1=xv[:, 1],
-                    op=ADD if sigma == 0 else SUB,
-                )
+            ni = 16 // parts
+            for k in range(parts):
+                for sigma in range(2):
+                    nc.vector.tensor_tensor(
+                        out=sdt[:, sigma, :, k * ni * 16:(k + 1) * ni * 16].rearrange("p v (i q) -> p v i q", q=16),
+                        in0=xv[:, 0, :, k * ni:(k + 1) * ni, :],
+                        in1=xv[:, 1, :, k * ni:(k + 1) * ni, :],
+                        op=ADD if sigma == 0 else SUB,
+                    )
 
         def prep_neg(hb):
             if ZMAP[hb]:
@@ -173,73 +190,112 @@ def tile_waveletlinearlayer_kernel(tc, x, W, b, out):
                 for sigma in range(2):
                     for u in range(2):
                         nc.tensor.transpose(bank[:, 2 * sigma + u, :], s[:, sigma, 2 * u + e, cols], ident[:])
-            e1s = e1p.tile([P, P, 4], F32, name="e1s")
-            nc.scalar.activation(out=e1s[:], in_=pb[:].rearrange("p k n -> p n k"), func=COPY, scale=0.5)
-            return (pa, e1s)
+            if gl == 0:
+                ev0 = e1p.tile([P, 2, P, 4], F32, name="ev0")
+                ev1 = e1p.tile([P, 2, P, 4], F32, name="ev1")
+                halves[hb] = (ev0, ev1)
+            ev0, ev1 = halves[hb]
+            nc.scalar.activation(out=ev1[:, gl], in_=pb[:].rearrange("p k n -> p n k"), func=COPY, scale=0.5)
+            nc.scalar.activation(out=ev0[:, gl], in_=pa[:].rearrange("p k n -> p n k"), func=COPY, scale=0.5)
+            return None
 
-        def combine(hb, gl, banks):
+        def combine(hb):
             bk, h = hb // H, hb % H
-            pa, e1s = banks
+            ev0, ev1 = halves[hb]
+            gv = grp[bk][:].rearrange("p (g a h c) -> p g a h c", g=2, a=2, h=H)
             for a in range(2):
-                nc.vector.scalar_tensor_tensor(
-                    out=gslice(bk, gl, a, h),
-                    in0=pa[:].rearrange("p k n -> p n k"),
-                    scalar=0.5,
-                    in1=e1s[:],
-                    op0=MULT,
-                    op1=ADD if a == 0 else SUB,
+                nc.vector.tensor_tensor(
+                    out=gv[:, :, a, h, :],
+                    in0=ev0[:].rearrange("p g n k -> p g (n k)"),
+                    in1=ev1[:].rearrange("p g n k -> p g (n k)"),
+                    op=ADD if a == 0 else SUB,
                 )
 
-        def t_quant(bk):
-            tcd = tqp.tile([P, 1024], U32, name="tcd", align_bytes=64)
-            tsc = tqp.tile([P, 1024], U8, name="tsc", align_bytes=64)
-            nc.vector.quantize_mx(out=tcd[:].bitcast(FP8X4), scales=tsc[:], in_=grp[bk][:])
-            tq[bk] = (tcd, tsc)
-            for gl in range(2):
-                for a in range(2):
-                    for h in range(H):
-                        pending.append((bk, gl, a, h))
+        def t_quant(bk, gl):
+            if gl == 0:
+                tcd = tqp.tile([P, 1024], U32, name="tcd", align_bytes=64)
+                tsc = tqp.tile([P, 1024], U8, name="tsc", align_bytes=64)
+                tq[bk] = (tcd, tsc)
+            tcd, tsc = tq[bk]
+            nc.vector.quantize_mx(
+                out=tcd[:, gl * 512:(gl + 1) * 512].bitcast(FP8X4),
+                scales=tsc[:, gl * 512:(gl + 1) * 512],
+                in_=grp[bk][:, gl * 2048:(gl + 1) * 2048],
+            )
+            for a in range(2):
+                for h in range(H):
+                    pending.append((bk, gl, a, h))
 
-        def passes(count):
+        opened = [0, 0]
+
+        def zero_passes(count):
+            for h in range(count):
+                nc.tensor.matmul_mx(
+                    out=acc[h][:],
+                    lhsT=zc[:, 0:P].bitcast(FP8X4),
+                    lhsT_scale=zs[:, 0:P],
+                    rhs=zc[:].bitcast(FP8X4),
+                    rhs_scale=zs[:],
+                    start=(opened[h] == 0),
+                    stop=False,
+                )
+                opened[h] = 1
+
+        def passes(count, tail):
+            if FILL and not tail and ripe[0] - cursor[0] < count:
+                zero_passes(count - (ripe[0] - cursor[0]))
             for k in range(min(count, ripe[0] - cursor[0])):
                 bk, gl, a, h = pending[cursor[0]]
                 cursor[0] = cursor[0] + 1
                 tcd, tsc = tq[bk]
+                narrow = tail or k >= WIDE
                 c0 = ((gl * 2 + a) * H + h) * P
-                w0 = (bk * 4 + gl * 2 + a) * OUT
+                nw = OUT if narrow else NW
+                w0 = (bk * 4 + gl * 2 + a) * OUT + NW - nw
                 nc.tensor.matmul_mx(
-                    out=acc[h][:],
+                    out=acc[h][:, NW - nw:NW],
                     lhsT=tcd[:, c0:c0 + P].bitcast(FP8X4),
                     lhsT_scale=tsc[:, c0:c0 + P],
-                    rhs=wc[:, w0:w0 + NW].bitcast(FP8X4),
-                    rhs_scale=ws[:, w0:w0 + NW],
-                    start=(bk == 0 and gl == 0 and a == 0),
+                    rhs=wc[:, w0:w0 + nw].bitcast(FP8X4),
+                    rhs_scale=ws[:, w0:w0 + nw],
+                    start=(opened[h] == 0),
                     stop=(bk == NBK - 1 and gl == 1 and a == 1),
                 )
+                opened[h] = 1
 
+        assert ZMAP[NHB - 1] == 1
         for hb in range(LEAD):
-            prep(hb)
-            prep_neg(hb)
+            prep(hb, 2 if hb == 0 else 1)
+            if hb < NL:
+                prep_neg(hb)
         for hb in range(NHB):
             bk, h = hb // H, hb % H
-            ripe[0] = len(pending)
+            last = hb == NHB - 1
+            ripe[0] = hist[hb - RL] if hb >= RL else 0
+            if hb > 0 and not ZMAP[hb - 1]:
+                combine(hb - 1)
             if hb + LEAD < NHB:
-                prep(hb + LEAD)
+                prep(hb + LEAD, 1)
             if h == 0 and bk > 0:
                 w_quant(bk - 1)
-                t_quant(bk - 1)
+                t_quant(bk - 1, 0)
+                t_quant(bk - 1, 1)
+            if last:
+                w_quant(bk)
             for gl in range(2):
-                banks = unit(hb, gl)
-                passes(PAIR)
-                if banks is not None:
-                    combine(hb, gl, banks)
-            w_front(bk, h)
-            if hb + LEAD < NHB:
-                prep_neg(hb + LEAD)
-        w_quant(NBK - 1)
-        t_quant(NBK - 1)
+                unit(hb, gl)
+                passes(PAIR, False)
+                if last:
+                    t_quant(bk, gl)
+            if hb == 0:
+                w_front(0, 0)
+            if not last:
+                w_front((hb + 1) // 2, (hb + 1) % 2)
+            if hb + NL < NHB:
+                prep_neg(hb + NL)
+            hist.append(len(pending))
         ripe[0] = len(pending)
-        passes(64)
+        passes(64, True)
 
         for h in range(H):
             res = const.tile([P, OUT], F32, name="res%d" % h)

@@ -24,14 +24,14 @@ NHB = NBK * H
 FLOPS = 2 * B * OUT * IN
 
 ZMAP = (1, 0, 1, 0, 1, 0, 1, 0, 1, 0, 1, 0, 1, 0, 0, 1)
-NW = 512
+NW = 128
 LEAD = 3
 PAIR = 2
 NEG_VECTOR = 0
 EB = 2
 RL = 2
 NL = 2
-FILL = 1
+FILL = 0
 WIDE = 2
 
 
@@ -98,8 +98,8 @@ def tile_waveletlinearlayer_kernel(tc, x, W, b, out):
         bias_sb = const.tile([P, OUT], BF16, name="bias_sb")
         nc.sync.dma_start(out=bias_sb[:], in_=b.partition_broadcast(P))
 
-        acc0 = accp.tile([P, NW], F32, name="acc0")
-        acc1 = accp.tile([P, NW], F32, name="acc1")
+        acc0 = accp.tile([P, 512], F32, name="acc0")
+        acc1 = accp.tile([P, 512], F32, name="acc1")
         acc = [acc0, acc1]
 
         sd = {}
@@ -271,7 +271,6 @@ def tile_waveletlinearlayer_kernel(tc, x, W, b, out):
         for hb in range(NHB):
             bk, h = hb // H, hb % H
             last = hb == NHB - 1
-            ripe[0] = hist[hb - RL] if hb >= RL else 0
             if hb > 0 and not ZMAP[hb - 1]:
                 combine(hb - 1)
             if hb + LEAD < NHB:
@@ -284,13 +283,15 @@ def tile_waveletlinearlayer_kernel(tc, x, W, b, out):
                 w_quant(bk)
             for gl in range(2):
                 unit(hb, gl)
-                passes(PAIR, False)
                 if last:
                     t_quant(bk, gl)
             if hb == 0:
                 w_front(0, 0)
             if not last:
                 w_front((hb + 1) // 2, (hb + 1) % 2)
+            if h == 1:
+                ripe[0] = hist[hb - 1]
+                passes(64, True)
             if hb + NL < NHB:
                 prep_neg(hb + NL)
             hist.append(len(pending))

@@ -5,13 +5,11 @@ from concourse.masks import make_identity
 
 F32 = mybir.dt.float32
 BF16 = mybir.dt.bfloat16
-I32 = mybir.dt.int32
 U32 = mybir.dt.uint32
 U8 = mybir.dt.uint8
 FP8X4 = mybir.dt.float8_e4m3fn_x4
 ADD = mybir.AluOpType.add
 SUB = mybir.AluOpType.subtract
-MULT = mybir.AluOpType.mult
 COPY = mybir.ActivationFunctionType.Copy
 
 P = 128
@@ -23,49 +21,36 @@ NBK = 8
 NHB = NBK * H
 FLOPS = 2 * B * OUT * IN
 
-ZMAP = (1, 0, 1, 0, 1, 0, 1, 0, 1, 0, 1, 0, 1, 0, 0, 1)
-NW = 128
 LEAD = 3
-PAIR = 2
-NEG_VECTOR = 0
-EB = 2
-RL = 2
-NL = 2
-FILL = 0
-WIDE = 2
+NL = 1
+NEGV = (1, 0)
+XB = 5
+RUN = 2
+PLAG = 4
 
 
 def tile_waveletlinearlayer_kernel(tc, x, W, b, out):
     nc = tc.nc
-    PAD = NW - OUT
     with ExitStack() as ctx:
         const = ctx.enter_context(tc.tile_pool(name="const", bufs=1))
         xin = ctx.enter_context(tc.tile_pool(name="xin", bufs=6))
         win = ctx.enter_context(tc.tile_pool(name="win", bufs=3))
         sdp = ctx.enter_context(tc.tile_pool(name="sdp", bufs=LEAD + 2))
-        e1p = ctx.enter_context(tc.tile_pool(name="e1p", bufs=EB))
-        grpp = ctx.enter_context(tc.tile_pool(name="grpp", bufs=2))
-        tqp = ctx.enter_context(tc.tile_pool(name="tqp", bufs=3))
+        nvp = ctx.enter_context(tc.tile_pool(name="nvp", bufs=LEAD + 2))
+        nsp = ctx.enter_context(tc.tile_pool(name="nsp", bufs=NL + 2))
+        grpp = ctx.enter_context(tc.tile_pool(name="grpp", bufs=5))
+        tqp = ctx.enter_context(tc.tile_pool(name="tqp", bufs=8))
         wgp = ctx.enter_context(tc.tile_pool(name="wgp", bufs=2))
         accp = ctx.enter_context(tc.psum_pool(name="accp", bufs=1))
-        xtp = ctx.enter_context(tc.psum_pool(name="xtp", bufs=2))
-        wtp = ctx.enter_context(tc.psum_pool(name="wtp", bufs=2))
+        xtp = ctx.enter_context(tc.psum_pool(name="xtp", bufs=XB))
+        wtp = ctx.enter_context(tc.psum_pool(name="wtp", bufs=1))
         ctx.enter_context(tc.manual_schedule())
 
         ident = const.tile([P, P], F32, name="ident")
         make_identity(nc, ident[:])
 
-        wc = const.tile([P, PAD + 32 * OUT], U32, name="wc", align_bytes=64)
-        ws = const.tile([P, PAD + 32 * OUT], U8, name="ws", align_bytes=64)
-        if PAD:
-            nc.vector.memset(wc[:, 0:PAD].bitcast(I32), 0)
-            nc.vector.memset(ws[:, 0:PAD].bitcast(I32), 0)
-        zc = const.tile([P, NW], U32, name="zc", align_bytes=64)
-        zs = const.tile([P, NW], U8, name="zs", align_bytes=64)
-        if FILL:
-            zb = const.tile([P, 4 * NW], BF16, name="zb", align_bytes=64)
-            nc.vector.memset(zb[:].bitcast(I32), 0)
-            nc.vector.quantize_mx(out=zc[:].bitcast(FP8X4), scales=zs[:], in_=zb[:])
+        wc = const.tile([P, 32 * OUT], U32, name="wc", align_bytes=64)
+        ws = const.tile([P, 32 * OUT], U8, name="ws", align_bytes=64)
 
         x_sb = {}
         w_sb = {}
@@ -86,8 +71,8 @@ def tile_waveletlinearlayer_kernel(tc, x, W, b, out):
 
         load_x(0, 2)
         load_x(1, 1)
-        load_x(2, 1)
         load_w(0)
+        load_x(2, 1)
         load_x(3, 1)
         for ch in range(1, C):
             load_x(4 * ch, 1)
@@ -107,11 +92,6 @@ def tile_waveletlinearlayer_kernel(tc, x, W, b, out):
         grp = {}
         tq = {}
         wgt = {}
-        halves = {}
-        pending = []
-        cursor = [0]
-        ripe = [0]
-        hist = []
 
         def prep(hb, parts):
             sdt = sdp.tile([P, 2, 4, 256], F32, name="sdt")
@@ -126,179 +106,131 @@ def tile_waveletlinearlayer_kernel(tc, x, W, b, out):
                         in1=xv[:, 1, :, k * ni:(k + 1) * ni, :],
                         op=ADD if sigma == 0 else SUB,
                     )
+                if parts > 1:
+                    prep_neg(hb, k)
 
-        def prep_neg(hb):
-            if ZMAP[hb]:
-                nst = sdp.tile([P, 2, 2, 256], F32, name="nst")
-                nsd[hb] = nst
-                odd = sd[hb][:].rearrange("p s (u e) c -> p s u e c", e=2)[:, :, :, 1, :]
-                if NEG_VECTOR:
-                    nc.vector.tensor_scalar_mul(out=nst[:], in0=odd, scalar1=-1.0)
-                else:
-                    nc.scalar.activation(out=nst[:], in_=odd, func=COPY, scale=-1.0)
+        def prep_neg(hb, gl):
+            nst = (nvp if NEGV[gl] else nsp).tile([P, 2, 2, P], F32, name="nst")
+            nsd[(hb, gl)] = nst
+            odd = sd[hb][:].rearrange("p s (u e) c -> p s u e c", e=2)[:, :, :, 1, gl * P:(gl + 1) * P]
+            if NEGV[gl]:
+                nc.vector.tensor_scalar_mul(out=nst[:], in0=odd, scalar1=-1.0)
+            else:
+                nc.scalar.activation(out=nst[:], in_=odd, func=COPY, scale=-1.0)
 
-        def w_front(bk, gl):
+        def w_front(j):
+            bk, gl = j // 2, j % 2
             ch, g = bk // 2, 2 * (bk % 2) + gl
-            if gl == 0:
-                wg = wgp.tile([P, 2048], BF16, name="wg", align_bytes=64)
-                wgt[bk] = wg
+            wg = wgp.tile([P, 1024], BF16, name="wg", align_bytes=64)
+            wgt[j] = wg
             wv = w_sb[ch][:].bitcast(F32)
-            wgv = wgt[bk][:].bitcast(F32).rearrange("p (g a o s) -> p g a o s", g=2, a=2, o=OUT, s=2)
             wT = wtp.tile([P, 4, OUT], F32, name="wT")
             for sub in range(4):
                 c0 = sub * 512 + g * P
                 nc.tensor.transpose(wT[:, sub, :], wv[:, c0:c0 + P], ident[:])
-            nc.scalar.copy(out=wgv[:, gl], in_=wT[:].rearrange("p (a s) o -> p a o s", a=2, s=2))
+            nc.scalar.copy(
+                out=wg[:].bitcast(F32).rearrange("p (a o s) -> p a o s", a=2, o=OUT, s=2),
+                in_=wT[:].rearrange("p (a s) o -> p a o s", a=2, s=2),
+            )
 
-        def w_quant(bk):
-            c0 = PAD + bk * 512
-            nc.vector.quantize_mx(out=wc[:, c0:c0 + 512].bitcast(FP8X4), scales=ws[:, c0:c0 + 512], in_=wgt[bk][:])
-
-        def gslice(bk, gl, a, h):
-            c0 = ((gl * 2 + a) * H + h) * 512
-            return grp[bk][:, c0:c0 + 512].rearrange("p (n k) -> p n k", k=4)
+        def w_quant(j):
+            c0 = j * 256
+            nc.vector.quantize_mx(out=wc[:, c0:c0 + 256].bitcast(FP8X4), scales=ws[:, c0:c0 + 256], in_=wgt[j][:])
 
         def unit(hb, gl):
-            bk, h = hb // H, hb % H
-            if h == 0 and gl == 0:
-                gt = grpp.tile([P, 4096], BF16, name="gt", align_bytes=64)
-                grp[bk] = gt
+            if gl == 0:
+                gt = grpp.tile([P, 2048], BF16, name="gt", align_bytes=64)
+                grp[hb] = gt
             cols = slice(gl * P, (gl + 1) * P)
-            pa = xtp.tile([P, 4, P], F32, name="pa")
-            pb = xtp.tile([P, 4, P], F32, name="pb")
             s = sd[hb]
-            if ZMAP[hb]:
-                for a in range(2):
-                    bank = pa if a == 0 else pb
-                    for sigma in range(2):
-                        for u in range(2):
-                            second = s[:, sigma, 2 * u + 1, cols] if a == 0 else nsd[hb][:, sigma, u, cols]
-                            nc.tensor.matmul(
-                                out=bank[:, 2 * sigma + u, :], lhsT=s[:, sigma, 2 * u, cols], rhs=ident[:],
-                                start=True, stop=False, is_transpose=True,
-                            )
-                            nc.tensor.matmul(
-                                out=bank[:, 2 * sigma + u, :], lhsT=second, rhs=ident[:],
-                                start=False, stop=True, is_transpose=True,
-                            )
-                    nc.scalar.activation(
-                        out=gslice(bk, gl, a, h), in_=bank[:].rearrange("p k n -> p n k"), func=COPY, scale=0.5,
-                    )
-                return None
-            for e in (1, 0):
-                bank = pa if e == 0 else pb
+            ns = nsd[(hb, gl)]
+            for a in range(2):
+                bank = xtp.tile([P, 4, P], F32, name="bank")
                 for sigma in range(2):
                     for u in range(2):
-                        nc.tensor.transpose(bank[:, 2 * sigma + u, :], s[:, sigma, 2 * u + e, cols], ident[:])
-            if gl == 0:
-                ev0 = e1p.tile([P, 2, P, 4], F32, name="ev0")
-                ev1 = e1p.tile([P, 2, P, 4], F32, name="ev1")
-                halves[hb] = (ev0, ev1)
-            ev0, ev1 = halves[hb]
-            nc.scalar.activation(out=ev1[:, gl], in_=pb[:].rearrange("p k n -> p n k"), func=COPY, scale=0.5)
-            nc.scalar.activation(out=ev0[:, gl], in_=pa[:].rearrange("p k n -> p n k"), func=COPY, scale=0.5)
-            return None
-
-        def combine(hb):
-            bk, h = hb // H, hb % H
-            ev0, ev1 = halves[hb]
-            gv = grp[bk][:].rearrange("p (g a h c) -> p g a h c", g=2, a=2, h=H)
-            for a in range(2):
-                nc.vector.tensor_tensor(
-                    out=gv[:, :, a, h, :],
-                    in0=ev0[:].rearrange("p g n k -> p g (n k)"),
-                    in1=ev1[:].rearrange("p g n k -> p g (n k)"),
-                    op=ADD if a == 0 else SUB,
+                        second = s[:, sigma, 2 * u + 1, cols] if a == 0 else ns[:, sigma, u, :]
+                        nc.tensor.matmul(
+                            out=bank[:, 2 * sigma + u, :], lhsT=s[:, sigma, 2 * u, cols], rhs=ident[:],
+                            start=True, stop=False, is_transpose=True,
+                        )
+                        nc.tensor.matmul(
+                            out=bank[:, 2 * sigma + u, :], lhsT=second, rhs=ident[:],
+                            start=False, stop=True, is_transpose=True,
+                        )
+                c0 = (gl * 2 + a) * 512
+                nc.scalar.activation(
+                    out=grp[hb][:, c0:c0 + 512].rearrange("p (n k) -> p n k", k=4),
+                    in_=bank[:].rearrange("p k n -> p n k"), func=COPY, scale=0.5,
                 )
 
-        def t_quant(bk, gl):
-            if gl == 0:
-                tcd = tqp.tile([P, 1024], U32, name="tcd", align_bytes=64)
-                tsc = tqp.tile([P, 1024], U8, name="tsc", align_bytes=64)
-                tq[bk] = (tcd, tsc)
-            tcd, tsc = tq[bk]
+        def t_quant(hb, parts):
+            tcd = tqp.tile([P, 512], U32, name="tcd", align_bytes=64)
+            tsc = tqp.tile([P, 512], U8, name="tsc", align_bytes=64)
+            tq[hb] = (tcd, tsc)
+            return [lambda k=k: t_quant_part(hb, parts, k) for k in range(parts)]
+
+        def t_quant_part(hb, parts, k):
+            tcd, tsc = tq[hb]
+            w = 512 // parts
             nc.vector.quantize_mx(
-                out=tcd[:, gl * 512:(gl + 1) * 512].bitcast(FP8X4),
-                scales=tsc[:, gl * 512:(gl + 1) * 512],
-                in_=grp[bk][:, gl * 2048:(gl + 1) * 2048],
+                out=tcd[:, k * w:(k + 1) * w].bitcast(FP8X4),
+                scales=tsc[:, k * w:(k + 1) * w],
+                in_=grp[hb][:, 4 * k * w:4 * (k + 1) * w],
             )
-            for a in range(2):
-                for h in range(H):
-                    pending.append((bk, gl, a, h))
 
-        opened = [0, 0]
-
-        def zero_passes(count):
-            for h in range(count):
-                nc.tensor.matmul_mx(
-                    out=acc[h][:],
-                    lhsT=zc[:, 0:P].bitcast(FP8X4),
-                    lhsT_scale=zs[:, 0:P],
-                    rhs=zc[:].bitcast(FP8X4),
-                    rhs_scale=zs[:],
-                    start=(opened[h] == 0),
-                    stop=False,
-                )
-                opened[h] = 1
-
-        def passes(count, tail):
-            if FILL and not tail and ripe[0] - cursor[0] < count:
-                zero_passes(count - (ripe[0] - cursor[0]))
-            for k in range(min(count, ripe[0] - cursor[0])):
-                bk, gl, a, h = pending[cursor[0]]
-                cursor[0] = cursor[0] + 1
-                tcd, tsc = tq[bk]
-                narrow = tail or k >= WIDE
-                c0 = ((gl * 2 + a) * H + h) * P
-                nw = OUT if narrow else NW
-                w0 = (bk * 4 + gl * 2 + a) * OUT + NW - nw
-                nc.tensor.matmul_mx(
-                    out=acc[h][:, NW - nw:NW],
-                    lhsT=tcd[:, c0:c0 + P].bitcast(FP8X4),
-                    lhsT_scale=tsc[:, c0:c0 + P],
-                    rhs=wc[:, w0:w0 + nw].bitcast(FP8X4),
-                    rhs_scale=ws[:, w0:w0 + nw],
-                    start=(opened[h] == 0),
-                    stop=(bk == NBK - 1 and gl == 1 and a == 1),
-                )
-                opened[h] = 1
-
-        assert ZMAP[NHB - 1] == 1
-        for hb in range(LEAD):
-            prep(hb, 2 if hb == 0 else 1)
-            if hb < NL:
-                prep_neg(hb)
-        for hb in range(NHB):
+        def passes(hb):
             bk, h = hb // H, hb % H
+            tcd, tsc = tq[hb]
+            for ga in range(4):
+                w0 = (bk * 4 + ga) * OUT
+                nc.tensor.matmul_mx(
+                    out=acc[h][:, 0:OUT],
+                    lhsT=tcd[:, ga * P:(ga + 1) * P].bitcast(FP8X4),
+                    lhsT_scale=tsc[:, ga * P:(ga + 1) * P],
+                    rhs=wc[:, w0:w0 + OUT].bitcast(FP8X4),
+                    rhs_scale=ws[:, w0:w0 + OUT],
+                    start=(bk == 0 and ga == 0),
+                    stop=(bk == NBK - 1 and ga == 3),
+                )
+
+        prep(0, 2)
+        for hb in range(1, LEAD):
+            prep(hb, 1)
+            prep_neg(hb, 0)
+        done = 0
+        for hb in range(NHB):
             last = hb == NHB - 1
-            if hb > 0 and not ZMAP[hb - 1]:
-                combine(hb - 1)
             if hb + LEAD < NHB:
                 prep(hb + LEAD, 1)
-            if h == 0 and bk > 0:
-                w_quant(bk - 1)
-                t_quant(bk - 1, 0)
-                t_quant(bk - 1, 1)
-            if last:
-                w_quant(bk)
-            for gl in range(2):
-                unit(hb, gl)
-                if last:
-                    t_quant(bk, gl)
-            if hb == 0:
-                w_front(0, 0)
-            if not last:
-                w_front((hb + 1) // 2, (hb + 1) % 2)
-            if h == 1:
-                ripe[0] = hist[hb - 1]
-                passes(64, True)
+            if hb > 0:
+                for part in t_quant(hb - 1, 1):
+                    part()
+                w_quant(hb - 1)
+            if hb + LEAD < NHB:
+                prep_neg(hb + LEAD, 0)
+            unit(hb, 0)
             if hb + NL < NHB:
-                prep_neg(hb + NL)
-            hist.append(len(pending))
-        ripe[0] = len(pending)
-        passes(64, True)
+                prep_neg(hb + NL, 1)
+            if last:
+                w_quant(hb)
+                parts = t_quant(hb, 2)
+                parts[0]()
+            unit(hb, 1)
+            if last:
+                parts[1]()
+            if hb == 0:
+                w_front(0)
+            if not last:
+                w_front(hb + 1)
+            if hb % RUN == 0:
+                while done <= hb - PLAG:
+                    passes(done)
+                    done += 1
+        while done < NHB:
+            passes(done)
+            done += 1
 
         for h in range(H):
             res = const.tile([P, OUT], F32, name="res%d" % h)
-            nc.vector.tensor_tensor(out=res[:], in0=acc[h][:, PAD:PAD + OUT], in1=bias_sb[:], op=ADD)
+            nc.vector.tensor_tensor(out=res[:], in0=acc[h][:, 0:OUT], in1=bias_sb[:], op=ADD)
             nc.sync.dma_start(out=out[h * P:(h + 1) * P, :], in_=res[:])

@@ -24,7 +24,7 @@ FLOPS = 2 * B * OUT * IN
 LEAD = 3
 NL = 1
 NEGV = (1, 0)
-XB = 5
+XB = 4
 RUN = 2
 PLAG = 4
 
@@ -40,10 +40,10 @@ def tile_waveletlinearlayer_kernel(tc, x, W, b, out):
         nsp = ctx.enter_context(tc.tile_pool(name="nsp", bufs=NL + 2))
         grpp = ctx.enter_context(tc.tile_pool(name="grpp", bufs=5))
         tqp = ctx.enter_context(tc.tile_pool(name="tqp", bufs=8))
-        wgp = ctx.enter_context(tc.tile_pool(name="wgp", bufs=2))
+        wgp = ctx.enter_context(tc.tile_pool(name="wgp", bufs=4))
         accp = ctx.enter_context(tc.psum_pool(name="accp", bufs=1))
         xtp = ctx.enter_context(tc.psum_pool(name="xtp", bufs=XB))
-        wtp = ctx.enter_context(tc.psum_pool(name="wtp", bufs=1))
+        wtp = ctx.enter_context(tc.psum_pool(name="wtp", bufs=2))
         ctx.enter_context(tc.manual_schedule())
 
         ident = const.tile([P, P], F32, name="ident")

@@ -209,8 +209,6 @@ def tile_waveletlinearlayer_kernel(tc, x, W, b, out):
             if hb + LEAD < NHB:
                 prep_neg(hb + LEAD, 0)
             unit(hb, 0)
-            if hb + NL < NHB:
-                prep_neg(hb + NL, 1)
             if last:
                 w_quant(hb)
                 parts = t_quant(hb, 2)
@@ -218,6 +216,8 @@ def tile_waveletlinearlayer_kernel(tc, x, W, b, out):
             unit(hb, 1)
             if last:
                 parts[1]()
+            if hb + NL < NHB:
+                prep_neg(hb + NL, 1)
             if hb == 0:
                 w_front(0)
             if not last:

@@ -27,6 +27,7 @@ NEGV = (1, 0)
 XB = 4
 RUN = 2
 PLAG = 4
+WARM = 6
 
 
 def tile_waveletlinearlayer_kernel(tc, x, W, b, out):
@@ -48,6 +49,12 @@ def tile_waveletlinearlayer_kernel(tc, x, W, b, out):
 
         ident = const.tile([P, P], F32, name="ident")
         make_identity(nc, ident[:])
+
+        zero = const.tile([P, P], F32, name="zero")
+        nc.vector.memset(zero[:], 0.0)
+        warm = xtp.tile([P, 4, P], F32, name="bank")
+        for k in range(WARM):
+            nc.tensor.matmul(out=warm[:, k % 4, :], lhsT=zero[:], rhs=zero[:], start=True, stop=True)
 
         wc = const.tile([P, 32 * OUT], U32, name="wc", align_bytes=64)
         ws = const.tile([P, 32 * OUT], U8, name="ws", align_bytes=64)

@@ -21,27 +21,45 @@ NBK = 8
 NHB = NBK * H
 FLOPS = 2 * B * OUT * IN
 
-LEAD = 3
+LEAD = 4
 NL = 1
 NEGV = (1, 0)
 XB = 4
 RUN = 2
-PLAG = 4
-WARM = 6
+PLAG = 7
+CATCH = {}
+GB = 5
+XI = 6
+WQ = 2
+VTAIL = 0
+EARLYRES = 0
+DB = 0
+DG = 1
+W0FIRST = 0
+WSEQ = ((0,), (2,), (3,), (1,), (4,), (5,), (6,), (7,), (8,), (9,), (10,), (11,), (12,), (13,), (14, 15), ())
+WQSEQ = {4: (1,), 5: (0,), 7: (2,), 9: (3,), 11: (4,), 13: (5,), 15: (6, 7)}
+WDV = 0
+XNEGV = (5,)
+NEGS = ()
+X0 = 1
+WARM = 4
+HNEG = 0
+WLEAD = 2
 
 
 def tile_waveletlinearlayer_kernel(tc, x, W, b, out):
     nc = tc.nc
     with ExitStack() as ctx:
         const = ctx.enter_context(tc.tile_pool(name="const", bufs=1))
-        xin = ctx.enter_context(tc.tile_pool(name="xin", bufs=6))
+        xin = ctx.enter_context(tc.tile_pool(name="xin", bufs=XI))
         win = ctx.enter_context(tc.tile_pool(name="win", bufs=3))
         sdp = ctx.enter_context(tc.tile_pool(name="sdp", bufs=LEAD + 2))
         nvp = ctx.enter_context(tc.tile_pool(name="nvp", bufs=LEAD + 2))
         nsp = ctx.enter_context(tc.tile_pool(name="nsp", bufs=NL + 2))
-        grpp = ctx.enter_context(tc.tile_pool(name="grpp", bufs=5))
-        tqp = ctx.enter_context(tc.tile_pool(name="tqp", bufs=8))
-        wgp = ctx.enter_context(tc.tile_pool(name="wgp", bufs=4))
+        grpp = ctx.enter_context(tc.tile_pool(name="grpp", bufs=GB))
+        tqp = ctx.enter_context(tc.tile_pool(name="tqp", bufs=PLAG + 3))
+        wgp = ctx.enter_context(tc.tile_pool(name="wgp", bufs=6 // WQ + 1))
+        xtsp = ctx.enter_context(tc.tile_pool(name="xtsp", bufs=2))
         accp = ctx.enter_context(tc.psum_pool(name="accp", bufs=1))
         xtp = ctx.enter_context(tc.psum_pool(name="xtp", bufs=XB))
         wtp = ctx.enter_context(tc.psum_pool(name="wtp", bufs=2))
@@ -55,6 +73,19 @@ def tile_waveletlinearlayer_kernel(tc, x, W, b, out):
         warm = xtp.tile([P, 4, P], F32, name="bank")
         for k in range(WARM):
             nc.tensor.matmul(out=warm[:, k % 4, :], lhsT=zero[:], rhs=zero[:], start=True, stop=True)
+
+        identb = const.tile([P, P], BF16, name="identb")
+        haar = const.tile([P, 4, 32], BF16, name="haar")
+        half = const.tile([P, 2, 64], F32, name="half")
+        nc.vector.tensor_copy(out=identb[:], in_=ident[:])
+        cols2 = ident[:].rearrange("p (c e) -> p e c", e=2)
+        for c in range(2):
+            op = ADD if c == 0 else SUB
+            nc.vector.tensor_tensor(out=half[:, c, :], in0=cols2[:, 0, :], in1=cols2[:, 1, :], op=op)
+        for c in range(2):
+            for r in range(2):
+                op = ADD if r == 0 else SUB
+                nc.vector.tensor_tensor(out=haar[:, 2 * c + r, :], in0=half[:, c, 0:32], in1=half[:, c, 32:64], op=op)
 
         wc = const.tile([P, 32 * OUT], U32, name="wc", align_bytes=64)
         ws = const.tile([P, 32 * OUT], U8, name="ws", align_bytes=64)
@@ -76,11 +107,43 @@ def tile_waveletlinearlayer_kernel(tc, x, W, b, out):
             nc.sync.dma_start(out=wt[:], in_=W[:, ch * CHW:(ch + 1) * CHW])
             w_sb[ch] = wt
 
-        load_x(0, 2)
-        load_x(1, 1)
-        load_w(0)
+        x0 = xin.tile([P, CHW // 2], BF16, name="xt")
+        x_sb[0] = x0
+        w0_sb = {}
+
+        def load_w0_group(g):
+            wt = win.tile([P, CHW // 4], BF16, name="w0t%d" % g, bufs=1)
+            w0_sb[g] = wt
+            nc.sync.dma_start(
+                out=wt[:].rearrange("p (s c) -> p s c", s=4),
+                in_=W[:, 0:CHW].rearrange("p (s g c) -> p g s c", s=4, g=4)[:, g],
+            )
+
+        wd = win.tile([P, 8, 4, 32], BF16, name="wd", bufs=1)
+
+        def load_wd():
+            ch, g = DB // 2, 2 * (DB % 2) + DG
+            for sub in range(4):
+                c0 = ch * CHW + sub * 1024 + g * 256
+                nc.sync.dma_start(
+                    out=wd[:, :, sub, :], in_=W[:, c0:c0 + 256].rearrange("p (i j) -> p i j", j=32),
+                )
+
+        for k in range(2):
+            for m in range(X0):
+                c0 = k * 1024 + m * 1024 // X0
+                c1 = c0 + 1024 // X0
+                nc.sync.dma_start(out=x0[:, c0:c1], in_=x[0:P, c0:c1])
+            if k == 0 and W0FIRST:
+                load_w0_group(0)
+        load_x(1, 2)
+        if not W0FIRST:
+            load_w0_group(0)
         load_x(2, 1)
+        load_w0_group(2)
+        load_w0_group(3)
         load_x(3, 1)
+        load_wd()
         for ch in range(1, C):
             load_x(4 * ch, 1)
             load_x(4 * ch + 1, 1)
@@ -100,12 +163,23 @@ def tile_waveletlinearlayer_kernel(tc, x, W, b, out):
         tq = {}
         wgt = {}
 
+        def dense(hb, gl):
+            return hb // H == DB and gl == DG
+
         def prep(hb, parts):
+            if hb // H == DB:
+                parts = 2 if hb else 2 * X0
+                if hb not in sd:
+                    prep_parts(hb, parts, range((1 - DG) * parts // 2, (2 - DG) * parts // 2))
+            else:
+                prep_parts(hb, parts, range(parts))
+
+        def prep_parts(hb, parts, ks):
             sdt = sdp.tile([P, 2, 4, 256], F32, name="sdt")
             sd[hb] = sdt
             xv = x_sb[hb][:].rearrange("p (i r q v) -> p r v i q", i=16, r=2, q=16, v=4)
             ni = 16 // parts
-            for k in range(parts):
+            for k in ks:
                 for sigma in range(2):
                     nc.vector.tensor_tensor(
                         out=sdt[:, sigma, :, k * ni * 16:(k + 1) * ni * 16].rearrange("p v (i q) -> p v i q", q=16),
@@ -113,14 +187,17 @@ def tile_waveletlinearlayer_kernel(tc, x, W, b, out):
                         in1=xv[:, 1, :, k * ni:(k + 1) * ni, :],
                         op=ADD if sigma == 0 else SUB,
                     )
-                if parts > 1:
-                    prep_neg(hb, k)
+                if hb == 0 and (k + 1) * 2 % parts == 0 and (HNEG or NEGV[(k + 1) * 2 // parts - 1]):
+                    prep_neg(hb, (k + 1) * 2 // parts - 1)
 
         def prep_neg(hb, gl):
-            nst = (nvp if NEGV[gl] else nsp).tile([P, 2, 2, P], F32, name="nst")
+            if dense(hb, gl) or (hb, gl) in nsd:
+                return
+            onv = (NEGV[gl] and hb not in NEGS) or (HNEG and hb == 0) or hb in XNEGV
+            nst = (nvp if onv else nsp).tile([P, 2, 2, P], F32, name="nst")
             nsd[(hb, gl)] = nst
             odd = sd[hb][:].rearrange("p s (u e) c -> p s u e c", e=2)[:, :, :, 1, gl * P:(gl + 1) * P]
-            if NEGV[gl]:
+            if onv:
                 nc.vector.tensor_scalar_mul(out=nst[:], in0=odd, scalar1=-1.0)
             else:
                 nc.scalar.activation(out=nst[:], in_=odd, func=COPY, scale=-1.0)
@@ -128,26 +205,65 @@ def tile_waveletlinearlayer_kernel(tc, x, W, b, out):
         def w_front(j):
             bk, gl = j // 2, j % 2
             ch, g = bk // 2, 2 * (bk % 2) + gl
-            wg = wgp.tile([P, 1024], BF16, name="wg", align_bytes=64)
-            wgt[j] = wg
-            wv = w_sb[ch][:].bitcast(F32)
+            if j - j % WQ not in wgt:
+                wg = wgp.tile([P, WQ * 1024], BF16, name="wg", align_bytes=64)
+                wgt[j - j % WQ] = wg
+            wg = wgt[j - j % WQ]
+            h0 = (j % WQ) * 1024
+            if dense(2 * bk, gl):
+                wTb = wtp.tile([P, 8, OUT], BF16, name="wT")
+                for i in range(8):
+                    nc.tensor.transpose(wTb[:, i, :], wd[:, i, :, :].rearrange("p s j -> p (s j)"), identb[:])
+                (nc.vector.tensor_copy if WDV else nc.scalar.copy)(
+                    out=wg[:, h0:h0 + 1024].rearrange("p (a o t) -> p a o t", a=2, o=OUT, t=4),
+                    in_=wTb[:].rearrange("p (a t) o -> p a o t", a=2, t=4),
+                )
+                return
+            wv = w0_sb[g][:].bitcast(F32) if ch == 0 else w_sb[ch][:].bitcast(F32)
             wT = wtp.tile([P, 4, OUT], F32, name="wT")
             for sub in range(4):
-                c0 = sub * 512 + g * P
+                c0 = sub * P if ch == 0 else sub * 512 + g * P
                 nc.tensor.transpose(wT[:, sub, :], wv[:, c0:c0 + P], ident[:])
             nc.scalar.copy(
-                out=wg[:].bitcast(F32).rearrange("p (a o s) -> p a o s", a=2, o=OUT, s=2),
+                out=wg[:, h0:h0 + 1024].bitcast(F32).rearrange("p (a o s) -> p a o s", a=2, o=OUT, s=2),
                 in_=wT[:].rearrange("p (a s) o -> p a o s", a=2, s=2),
             )
 
         def w_quant(j):
-            c0 = j * 256
-            nc.vector.quantize_mx(out=wc[:, c0:c0 + 256].bitcast(FP8X4), scales=ws[:, c0:c0 + 256], in_=wgt[j][:])
+            if (j + 1) % WQ:
+                return
+            j0 = j + 1 - WQ
+            c0, c1 = j0 * 256, (j + 1) * 256
+            nc.vector.quantize_mx(out=wc[:, c0:c1].bitcast(FP8X4), scales=ws[:, c0:c1], in_=wgt[j0][:])
+
+        xts = {}
+
+        def raw(hb):
+            bankr = xtp.tile([P, 8, P], BF16, name="bank")
+            for i in range(8):
+                c0 = DG * 1024 + i * P
+                nc.tensor.transpose(bankr[:, i, :], x_sb[hb][:, c0:c0 + P], identb[:])
+            xt = xtsp.tile([P, 8, P], BF16, name="xT")
+            xts[hb] = xt
+            nc.scalar.copy(out=xt[:], in_=bankr[:])
 
         def unit(hb, gl):
-            if gl == 0:
+            if hb not in grp:
                 gt = grpp.tile([P, 2048], BF16, name="gt", align_bytes=64)
                 grp[hb] = gt
+            if dense(hb, gl):
+                for a in range(2):
+                    bank = xtp.tile([P, 4, P], F32, name="bank")
+                    nc.tensor.matmul(
+                        out=bank[:].rearrange("p k n -> p (k n)"), lhsT=haar[:].rearrange("p s j -> p (s j)"),
+                        rhs=xts[hb][:, 4 * a:4 * a + 4, :].rearrange("p k n -> p (k n)"), start=True, stop=True,
+                    )
+                    c0 = (gl * 2 + a) * 512
+                    nc.scalar.activation(
+                        out=grp[hb][:, c0:c0 + 512].rearrange("p (n k) -> p n k", k=4),
+                        in_=bank[:].rearrange("p k n -> p n k"), func=COPY, scale=0.5,
+                    )
+                return
             cols = slice(gl * P, (gl + 1) * P)
             s = sd[hb]
             ns = nsd[(hb, gl)]
@@ -165,6 +281,12 @@ def tile_waveletlinearlayer_kernel(tc, x, W, b, out):
                             start=False, stop=True, is_transpose=True,
                         )
                 c0 = (gl * 2 + a) * 512
+                if hb == NHB - 1 and gl * 2 + a >= 4 - VTAIL:
+                    nc.vector.tensor_scalar_mul(
+                        out=grp[hb][:, c0:c0 + 512].rearrange("p (n k) -> p n k", k=4),
+                        in0=bank[:].rearrange("p k n -> p n k"), scalar1=0.5,
+                    )
+                    continue
                 nc.scalar.activation(
                     out=grp[hb][:, c0:c0 + 512].rearrange("p (n k) -> p n k", k=4),
                     in_=bank[:].rearrange("p k n -> p n k"), func=COPY, scale=0.5,
@@ -200,11 +322,14 @@ def tile_waveletlinearlayer_kernel(tc, x, W, b, out):
                     stop=(bk == NBK - 1 and ga == 3),
                 )
 
-        prep(0, 2)
+        prep(0, 2 * X0)
         for hb in range(1, LEAD):
             prep(hb, 1)
             prep_neg(hb, 0)
+            if hb in XNEGV:
+                prep_neg(hb, 1)
         done = 0
+        wdone = 0
         for hb in range(NHB):
             last = hb == NHB - 1
             if hb + LEAD < NHB:
@@ -212,25 +337,37 @@ def tile_waveletlinearlayer_kernel(tc, x, W, b, out):
             if hb > 0:
                 for part in t_quant(hb - 1, 1):
                     part()
-                w_quant(hb - 1)
-            if hb + LEAD < NHB:
+            for j in WQSEQ.get(hb, ()):
+                w_quant(2 * j + 1)
+            if hb + LEAD < NHB and hb + LEAD not in NEGS:
                 prep_neg(hb + LEAD, 0)
+            if hb + LEAD < NHB and hb + LEAD in XNEGV:
+                prep_neg(hb + LEAD, 1)
+            if hb == 0:
+                if W0FIRST:
+                    w_front(0)
+                    wdone = 1
+                if DB == 0:
+                    raw(0)
+            if DB and (hb + 1) // H == DB:
+                raw(hb + 1)
             unit(hb, 0)
+            if hb == 0 and DB == 0:
+                raw(1)
             if last:
-                w_quant(hb)
                 parts = t_quant(hb, 2)
                 parts[0]()
             unit(hb, 1)
             if last:
                 parts[1]()
             if hb + NL < NHB:
+                if hb + NL in NEGS:
+                    prep_neg(hb + NL, 0)
                 prep_neg(hb + NL, 1)
-            if hb == 0:
-                w_front(0)
-            if not last:
-                w_front(hb + 1)
+            for j in WSEQ[hb]:
+                w_front(j)
             if hb % RUN == 0:
-                while done <= hb - PLAG:
+                while done <= CATCH.get(hb, hb - PLAG):
                     passes(done)
                     done += 1
         while done < NHB:

@@ -26,18 +26,21 @@ NL = 1
 NEGV = (1, 0)
 XB = 4
 RUN = 2
-PLAG = 7
+PLAG = 6
 CATCH = {}
+SK = ()
 GB = 5
-XI = 6
+XI = 8
 WQ = 2
 VTAIL = 0
 EARLYRES = 0
 DB = 0
 DG = 1
 W0FIRST = 0
-WSEQ = ((0,), (2,), (3,), (1,), (4,), (5,), (6,), (7,), (8,), (9,), (10,), (11,), (12,), (13,), (14, 15), ())
-WQSEQ = {4: (1,), 5: (0,), 7: (2,), 9: (3,), 11: (4,), 13: (5,), 15: (6, 7)}
+WSEQ = ((), (2,), (3,), (4,), (5,), (6,), (7,), (8,), (9,), (10,), (11,), (0, 1), (12, 13), (14,), (15,), ())
+WQSEQ = {4: (1,), 6: (2,), 8: (3,), 10: (4,), 12: (5,), 13: (0,), 14: (6,), 15: (7,)}
+ORDER = (2, 3, 4, 5, 6, 7, 8, 9, 10, 11, 0, 1, 12, 13, 14, 15)
+LOADS = (("x", 2), ("w", 2, 2), ("x", 3), ("x", 4), ("w", 4, 2), ("x", 5), ("x", 6), ("w", 6, 2), ("x", 7), ("x", 8), ("w", 8, 4), ("x", 9), ("x", 10), "d", ("w", 0, 1), ("x", 11), ("w", 12, 4), ("x", 12), ("x", 13), ("x", 14), ("x", 15))
 WDV = 0
 XNEGV = (5,)
 NEGS = ()
@@ -52,7 +55,7 @@ def tile_waveletlinearlayer_kernel(tc, x, W, b, out):
     with ExitStack() as ctx:
         const = ctx.enter_context(tc.tile_pool(name="const", bufs=1))
         xin = ctx.enter_context(tc.tile_pool(name="xin", bufs=XI))
-        win = ctx.enter_context(tc.tile_pool(name="win", bufs=3))
+        win = ctx.enter_context(tc.tile_pool(name="win", bufs=2))
         sdp = ctx.enter_context(tc.tile_pool(name="sdp", bufs=LEAD + 2))
         nvp = ctx.enter_context(tc.tile_pool(name="nvp", bufs=LEAD + 2))
         nsp = ctx.enter_context(tc.tile_pool(name="nsp", bufs=NL + 2))
@@ -93,63 +96,41 @@ def tile_waveletlinearlayer_kernel(tc, x, W, b, out):
         x_sb = {}
         w_sb = {}
 
-        def load_x(hb, parts):
+        def load_x(hb, c0, c1):
             bk, h = hb // H, hb % H
-            xt = xin.tile([P, CHW // 2], BF16, name="xt")
-            w = CHW // 2 // parts
-            for k in range(parts):
-                c0 = bk * (CHW // 2) + k * w
-                nc.sync.dma_start(out=xt[:, k * w:(k + 1) * w], in_=x[h * P:(h + 1) * P, c0:c0 + w])
-            x_sb[hb] = xt
+            if hb not in x_sb:
+                xt = xin.tile([P, CHW // 2], BF16, name="xt")
+                x_sb[hb] = xt
+            o = bk * (CHW // 2)
+            nc.sync.dma_start(out=x_sb[hb][:, c0:c1], in_=x[h * P:(h + 1) * P, o + c0:o + c1])
 
-        def load_w(ch):
-            wt = win.tile([P, CHW], BF16, name="wt")
-            nc.sync.dma_start(out=wt[:], in_=W[:, ch * CHW:(ch + 1) * CHW])
-            w_sb[ch] = wt
-
-        x0 = xin.tile([P, CHW // 2], BF16, name="xt")
-        x_sb[0] = x0
-        w0_sb = {}
-
-        def load_w0_group(g):
-            wt = win.tile([P, CHW // 4], BF16, name="w0t%d" % g, bufs=1)
-            w0_sb[g] = wt
-            nc.sync.dma_start(
-                out=wt[:].rearrange("p (s c) -> p s c", s=4),
-                in_=W[:, 0:CHW].rearrange("p (s g c) -> p g s c", s=4, g=4)[:, g],
-            )
+        def load_w(j, n):
+            ch, g = j // 4, j % 4
+            wt = win.tile([P, 4, n * 256], BF16, name="wt%d" % n)
+            for k in range(n):
+                w_sb[j + k] = (wt, k * P)
+            w4 = W[:, ch * CHW:(ch + 1) * CHW].rearrange("p (s c) -> p s c", s=4)
+            nc.sync.dma_start(out=wt[:], in_=w4[:, :, g * 256:(g + n) * 256])
 
         wd = win.tile([P, 8, 4, 32], BF16, name="wd", bufs=1)
 
         def load_wd():
-            ch, g = DB // 2, 2 * (DB % 2) + DG
             for sub in range(4):
-                c0 = ch * CHW + sub * 1024 + g * 256
-                nc.sync.dma_start(
-                    out=wd[:, :, sub, :], in_=W[:, c0:c0 + 256].rearrange("p (i j) -> p i j", j=32),
-                )
+                c0 = sub * 1024 + DG * 256
+                nc.sync.dma_start(out=wd[:, :, sub, :], in_=W[:, c0:c0 + 256].rearrange("p (i j) -> p i j", j=32))
 
-        for k in range(2):
-            for m in range(X0):
-                c0 = k * 1024 + m * 1024 // X0
-                c1 = c0 + 1024 // X0
-                nc.sync.dma_start(out=x0[:, c0:c1], in_=x[0:P, c0:c1])
-            if k == 0 and W0FIRST:
-                load_w0_group(0)
-        load_x(1, 2)
-        if not W0FIRST:
-            load_w0_group(0)
-        load_x(2, 1)
-        load_w0_group(2)
-        load_w0_group(3)
-        load_x(3, 1)
-        load_wd()
-        for ch in range(1, C):
-            load_x(4 * ch, 1)
-            load_x(4 * ch + 1, 1)
-            load_w(ch)
-            load_x(4 * ch + 2, 1)
-            load_x(4 * ch + 3, 1)
+        for hb in range(H):
+            for m in range(X0 if hb == 0 else 1):
+                n = X0 if hb == 0 else 1
+                load_x(hb, (1 - DG) * 1024 + m * 1024 // n, (1 - DG) * 1024 + (m + 1) * 1024 // n)
+            load_x(hb, DG * 1024, DG * 1024 + 1024)
+        for item in LOADS:
+            if item == "d":
+                load_wd()
+            elif item[0] == "x":
+                load_x(item[1], 0, 2048)
+            else:
+                load_w(item[1], item[2])
         bias_sb = const.tile([P, OUT], BF16, name="bias_sb")
         nc.sync.dma_start(out=bias_sb[:], in_=b.partition_broadcast(P))
 
@@ -219,11 +200,10 @@ def tile_waveletlinearlayer_kernel(tc, x, W, b, out):
                     in_=wTb[:].rearrange("p (a t) o -> p a o t", a=2, t=4),
                 )
                 return
-            wv = w0_sb[g][:].bitcast(F32) if ch == 0 else w_sb[ch][:].bitcast(F32)
+            wt, wo = w_sb[j]
             wT = wtp.tile([P, 4, OUT], F32, name="wT")
             for sub in range(4):
-                c0 = sub * P if ch == 0 else sub * 512 + g * P
-                nc.tensor.transpose(wT[:, sub, :], wv[:, c0:c0 + P], ident[:])
+                nc.tensor.transpose(wT[:, sub, :], wt[:, sub, :].bitcast(F32)[:, wo:wo + P], ident[:])
             nc.scalar.copy(
                 out=wg[:, h0:h0 + 1024].bitcast(F32).rearrange("p (a o s) -> p a o s", a=2, o=OUT, s=2),
                 in_=wT[:].rearrange("p (a s) o -> p a o s", a=2, s=2),
@@ -318,8 +298,8 @@ def tile_waveletlinearlayer_kernel(tc, x, W, b, out):
                     lhsT_scale=tsc[:, ga * P:(ga + 1) * P],
                     rhs=wc[:, w0:w0 + OUT].bitcast(FP8X4),
                     rhs_scale=ws[:, w0:w0 + OUT],
-                    start=(bk == 0 and ga == 0),
-                    stop=(bk == NBK - 1 and ga == 3),
+                    start=(hb in (ORDER[0], ORDER[1]) and ga == 0),
+                    stop=(hb in (ORDER[-1], ORDER[-2]) and ga == 3),
                 )
 
         prep(0, 2 * X0)
@@ -329,24 +309,25 @@ def tile_waveletlinearlayer_kernel(tc, x, W, b, out):
             if hb in XNEGV:
                 prep_neg(hb, 1)
         done = 0
-        wdone = 0
+        nxt = LEAD
         for hb in range(NHB):
             last = hb == NHB - 1
-            if hb + LEAD < NHB:
-                prep(hb + LEAD, 1)
+            nx = nxt if hb not in SK else NHB
+            if nx < NHB:
+                prep(nx, 1)
+                nxt += 1
             if hb > 0:
                 for part in t_quant(hb - 1, 1):
                     part()
             for j in WQSEQ.get(hb, ()):
                 w_quant(2 * j + 1)
-            if hb + LEAD < NHB and hb + LEAD not in NEGS:
-                prep_neg(hb + LEAD, 0)
-            if hb + LEAD < NHB and hb + LEAD in XNEGV:
-                prep_neg(hb + LEAD, 1)
+            if nx < NHB and nx not in NEGS:
+                prep_neg(nx, 0)
+            if nx < NHB and nx in XNEGV:
+                prep_neg(nx, 1)
             if hb == 0:
                 if W0FIRST:
                     w_front(0)
-                    wdone = 1
                 if DB == 0:
                     raw(0)
             if DB and (hb + 1) // H == DB:
@@ -367,11 +348,11 @@ def tile_waveletlinearlayer_kernel(tc, x, W, b, out):
             for j in WSEQ[hb]:
                 w_front(j)
             if hb % RUN == 0:
-                while done <= CATCH.get(hb, hb - PLAG):
-                    passes(done)
+                while done < CATCH.get(hb, hb - PLAG):
+                    passes(ORDER[done])
                     done += 1
         while done < NHB:
-            passes(done)
+            passes(ORDER[done])
             done += 1
 
         for h in range(H):

@@ -10,6 +10,7 @@ U8 = mybir.dt.uint8
 FP8X4 = mybir.dt.float8_e4m3fn_x4
 ADD = mybir.AluOpType.add
 SUB = mybir.AluOpType.subtract
+MULT = mybir.AluOpType.mult
 COPY = mybir.ActivationFunctionType.Copy
 
 P = 128
@@ -23,31 +24,29 @@ FLOPS = 2 * B * OUT * IN
 
 LEAD = 4
 NL = 1
-NEGV = (1, 0)
+VNEG = (1, 1, 2, 0, 2, 0, 1, 0, 2, 0, 1, 0, 2, 0, 1, 0)
 XB = 4
 RUN = 2
 PLAG = 6
 CATCH = {}
 SK = ()
-GB = 5
+NAT = ((6, 1), (10, 1), (14, 1))
+GB = 3
+TB = 5
+TQSEQ = {2: 0, 4: 2, 6: 4, 8: 6, 10: 8, 12: 10, 14: 12}
+HEADX = ((0, 512), (1024, 1536), (512, 1024), (1536, 2048))
 XI = 8
 WQ = 2
 VTAIL = 0
-EARLYRES = 0
 DB = 0
 DG = 1
-W0FIRST = 0
 WSEQ = ((), (2,), (3,), (4,), (5,), (6,), (7,), (8,), (9,), (10,), (11,), (0, 1), (12, 13), (14,), (15,), ())
 WQSEQ = {4: (1,), 6: (2,), 8: (3,), 10: (4,), 12: (5,), 13: (0,), 14: (6,), 15: (7,)}
 ORDER = (2, 3, 4, 5, 6, 7, 8, 9, 10, 11, 0, 1, 12, 13, 14, 15)
 LOADS = (("x", 2), ("w", 2, 2), ("x", 3), ("x", 4), ("w", 4, 2), ("x", 5), ("x", 6), ("w", 6, 2), ("x", 7), ("x", 8), ("w", 8, 4), ("x", 9), ("x", 10), "d", ("w", 0, 1), ("x", 11), ("w", 12, 4), ("x", 12), ("x", 13), ("x", 14), ("x", 15))
 WDV = 0
-XNEGV = (5,)
-NEGS = ()
-X0 = 1
+X0 = 2
 WARM = 4
-HNEG = 0
-WLEAD = 2
 
 
 def tile_waveletlinearlayer_kernel(tc, x, W, b, out):
@@ -57,12 +56,13 @@ def tile_waveletlinearlayer_kernel(tc, x, W, b, out):
         xin = ctx.enter_context(tc.tile_pool(name="xin", bufs=XI))
         win = ctx.enter_context(tc.tile_pool(name="win", bufs=2))
         sdp = ctx.enter_context(tc.tile_pool(name="sdp", bufs=LEAD + 2))
-        nvp = ctx.enter_context(tc.tile_pool(name="nvp", bufs=LEAD + 2))
+        nvp = ctx.enter_context(tc.tile_pool(name="nvp", bufs=4))
         nsp = ctx.enter_context(tc.tile_pool(name="nsp", bufs=NL + 2))
+        natp = ctx.enter_context(tc.tile_pool(name="natp", bufs=4))
         grpp = ctx.enter_context(tc.tile_pool(name="grpp", bufs=GB))
-        tqp = ctx.enter_context(tc.tile_pool(name="tqp", bufs=PLAG + 3))
+        tqp = ctx.enter_context(tc.tile_pool(name="tqp", bufs=TB))
         wgp = ctx.enter_context(tc.tile_pool(name="wgp", bufs=6 // WQ + 1))
-        xtsp = ctx.enter_context(tc.tile_pool(name="xtsp", bufs=2))
+        xtsp = ctx.enter_context(tc.tile_pool(name="xtsp", bufs=4))
         accp = ctx.enter_context(tc.psum_pool(name="accp", bufs=1))
         xtp = ctx.enter_context(tc.psum_pool(name="xtp", bufs=XB))
         wtp = ctx.enter_context(tc.psum_pool(name="wtp", bufs=2))
@@ -106,7 +106,7 @@ def tile_waveletlinearlayer_kernel(tc, x, W, b, out):
 
         def load_w(j, n):
             ch, g = j // 4, j % 4
-            wt = win.tile([P, 4, n * 256], BF16, name="wt%d" % n)
+            wt = win.tile([P, 4, n * 256], BF16, name="wt%d" % n, bufs=2 if n > 1 else 1)
             for k in range(n):
                 w_sb[j + k] = (wt, k * P)
             w4 = W[:, ch * CHW:(ch + 1) * CHW].rearrange("p (s c) -> p s c", s=4)
@@ -119,11 +119,10 @@ def tile_waveletlinearlayer_kernel(tc, x, W, b, out):
                 c0 = sub * 1024 + DG * 256
                 nc.sync.dma_start(out=wd[:, :, sub, :], in_=W[:, c0:c0 + 256].rearrange("p (i j) -> p i j", j=32))
 
-        for hb in range(H):
-            for m in range(X0 if hb == 0 else 1):
-                n = X0 if hb == 0 else 1
-                load_x(hb, (1 - DG) * 1024 + m * 1024 // n, (1 - DG) * 1024 + (m + 1) * 1024 // n)
-            load_x(hb, DG * 1024, DG * 1024 + 1024)
+        for c0, c1 in HEADX:
+            load_x(0, c0, c1)
+        load_x(1, 0, 1024)
+        load_x(1, 1024, 2048)
         for item in LOADS:
             if item == "d":
                 load_wd()
@@ -141,7 +140,9 @@ def tile_waveletlinearlayer_kernel(tc, x, W, b, out):
         sd = {}
         nsd = {}
         grp = {}
+        gpair = {}
         tq = {}
+        tpair = {}
         wgt = {}
 
         def dense(hb, gl):
@@ -168,20 +169,38 @@ def tile_waveletlinearlayer_kernel(tc, x, W, b, out):
                         in1=xv[:, 1, :, k * ni:(k + 1) * ni, :],
                         op=ADD if sigma == 0 else SUB,
                     )
-                if hb == 0 and (k + 1) * 2 % parts == 0 and (HNEG or NEGV[(k + 1) * 2 // parts - 1]):
-                    prep_neg(hb, (k + 1) * 2 // parts - 1)
 
-        def prep_neg(hb, gl):
-            if dense(hb, gl) or (hb, gl) in nsd:
-                return
-            onv = (NEGV[gl] and hb not in NEGS) or (HNEG and hb == 0) or hb in XNEGV
-            nst = (nvp if onv else nsp).tile([P, 2, 2, P], F32, name="nst")
-            nsd[(hb, gl)] = nst
-            odd = sd[hb][:].rearrange("p s (u e) c -> p s u e c", e=2)[:, :, :, 1, gl * P:(gl + 1) * P]
+        def prep_neg(hb, g0, g1, onv):
+            n = (g1 - g0) * P
+            nst = (nvp if onv else nsp).tile([P, 2, 2, n], F32, name="nst%d" % n)
+            for gl in range(g0, g1):
+                nsd[(hb, gl)] = nst[:, :, :, (gl - g0) * P:(gl - g0 + 1) * P]
+            odd = sd[hb][:].rearrange("p s (u e) c -> p s u e c", e=2)[:, :, :, 1, g0 * P:g1 * P]
             if onv:
                 nc.vector.tensor_scalar_mul(out=nst[:], in0=odd, scalar1=-1.0)
             else:
                 nc.scalar.activation(out=nst[:], in_=odd, func=COPY, scale=-1.0)
+
+        nat = {}
+
+        def natural(hb, gl):
+            nt = natp.tile([P, 2, P, 2], BF16, name="nt")
+            nat[(hb, gl)] = nt
+            v = sd[hb][:].rearrange("p s (u e) c -> p s c u e", e=2)[:, :, gl * P:(gl + 1) * P]
+            nc.vector.tensor_tensor(out=nt[:], in0=v[:, :, :, :, 0], in1=v[:, :, :, :, 1], op=SUB)
+
+        def neg_v(hb):
+            for gl in range(2):
+                if (hb, gl) in NAT:
+                    natural(hb, gl)
+            if hb < 2:
+                prep_neg(hb, 0, 1, True)
+            elif VNEG[hb]:
+                prep_neg(hb, 0, VNEG[hb], True)
+
+        def neg_s(hb, gl):
+            if 2 <= hb < NHB and VNEG[hb] <= gl and (hb, gl) not in NAT:
+                prep_neg(hb, gl, gl + 1, False)
 
         def w_front(j):
             bk, gl = j // 2, j % 2
@@ -218,40 +237,51 @@ def tile_waveletlinearlayer_kernel(tc, x, W, b, out):
 
         xts = {}
 
-        def raw(hb):
-            bankr = xtp.tile([P, 8, P], BF16, name="bank")
-            for i in range(8):
-                c0 = DG * 1024 + i * P
+        def raw(hb, a):
+            bankr = xtp.tile([P, 4, P], BF16, name="bank")
+            for i in range(4):
+                c0 = DG * 1024 + (4 * a + i) * P
                 nc.tensor.transpose(bankr[:, i, :], x_sb[hb][:, c0:c0 + P], identb[:])
-            xt = xtsp.tile([P, 8, P], BF16, name="xT")
-            xts[hb] = xt
+            xt = xtsp.tile([P, 4, P], BF16, name="xT")
+            xts[(hb, a)] = xt
             nc.scalar.copy(out=xt[:], in_=bankr[:])
 
         def unit(hb, gl):
             if hb not in grp:
-                gt = grpp.tile([P, 2048], BF16, name="gt", align_bytes=64)
-                grp[hb] = gt
+                gt = grpp.tile([P, 4096], BF16, name="gt", align_bytes=64)
+                grp[hb] = gt[:, 0:2048]
+                grp[hb + 1] = gt[:, 2048:4096]
+                gpair[hb] = gt
             if dense(hb, gl):
                 for a in range(2):
                     bank = xtp.tile([P, 4, P], F32, name="bank")
                     nc.tensor.matmul(
                         out=bank[:].rearrange("p k n -> p (k n)"), lhsT=haar[:].rearrange("p s j -> p (s j)"),
-                        rhs=xts[hb][:, 4 * a:4 * a + 4, :].rearrange("p k n -> p (k n)"), start=True, stop=True,
+                        rhs=xts[(hb, a)][:].rearrange("p k n -> p (k n)"), start=True, stop=True,
                     )
                     c0 = (gl * 2 + a) * 512
                     nc.scalar.activation(
                         out=grp[hb][:, c0:c0 + 512].rearrange("p (n k) -> p n k", k=4),
-                        in_=bank[:].rearrange("p k n -> p n k"), func=COPY, scale=0.5,
+                        in_=bank[:].rearrange("p k n -> p n k"), func=COPY, scale=1.0,
                     )
                 return
             cols = slice(gl * P, (gl + 1) * P)
             s = sd[hb]
-            ns = nsd[(hb, gl)]
             for a in range(2):
                 bank = xtp.tile([P, 4, P], F32, name="bank")
+                if a == 1 and (hb, gl) in nat:
+                    nt = nat[(hb, gl)][:].rearrange("p s c u -> p s (c u)")
+                    for sigma in range(2):
+                        nc.tensor.transpose(bank[:, sigma, :], nt[:, sigma, :].bitcast(F32), ident[:])
+                    c0 = (gl * 2 + a) * 512
+                    nc.scalar.copy(
+                        out=grp[hb][:, c0:c0 + 512].bitcast(F32).rearrange("p (n k) -> p n k", k=2),
+                        in_=bank[:, 0:2, :].rearrange("p k n -> p n k"),
+                    )
+                    continue
                 for sigma in range(2):
                     for u in range(2):
-                        second = s[:, sigma, 2 * u + 1, cols] if a == 0 else ns[:, sigma, u, :]
+                        second = s[:, sigma, 2 * u + 1, cols] if a == 0 else nsd[(hb, gl)][:, sigma, u, :]
                         nc.tensor.matmul(
                             out=bank[:, 2 * sigma + u, :], lhsT=s[:, sigma, 2 * u, cols], rhs=ident[:],
                             start=True, stop=False, is_transpose=True,
@@ -264,27 +294,28 @@ def tile_waveletlinearlayer_kernel(tc, x, W, b, out):
                 if hb == NHB - 1 and gl * 2 + a >= 4 - VTAIL:
                     nc.vector.tensor_scalar_mul(
                         out=grp[hb][:, c0:c0 + 512].rearrange("p (n k) -> p n k", k=4),
-                        in0=bank[:].rearrange("p k n -> p n k"), scalar1=0.5,
+                        in0=bank[:].rearrange("p k n -> p n k"), scalar1=1.0,
                     )
                     continue
                 nc.scalar.activation(
                     out=grp[hb][:, c0:c0 + 512].rearrange("p (n k) -> p n k", k=4),
-                    in_=bank[:].rearrange("p k n -> p n k"), func=COPY, scale=0.5,
+                    in_=bank[:].rearrange("p k n -> p n k"), func=COPY, scale=1.0,
                 )
 
-        def t_quant(hb, parts):
-            tcd = tqp.tile([P, 512], U32, name="tcd", align_bytes=64)
-            tsc = tqp.tile([P, 512], U8, name="tsc", align_bytes=64)
-            tq[hb] = (tcd, tsc)
-            return [lambda k=k: t_quant_part(hb, parts, k) for k in range(parts)]
-
-        def t_quant_part(hb, parts, k):
-            tcd, tsc = tq[hb]
-            w = 512 // parts
+        def t_quant(b0, b1):
+            hb = b0 // 8 * 2
+            if hb not in tq:
+                tcd = tqp.tile([P, 1024], U32, name="tcd", align_bytes=64)
+                tsc = tqp.tile([P, 1024], U8, name="tsc", align_bytes=64)
+                tq[hb] = (tcd[:, 0:512], tsc[:, 0:512])
+                tq[hb + 1] = (tcd[:, 512:1024], tsc[:, 512:1024])
+                tpair[hb] = (tcd, tsc)
+            tcd, tsc = tpair[hb]
+            k0, k1 = b0 - 4 * hb, b1 - 4 * hb
             nc.vector.quantize_mx(
-                out=tcd[:, k * w:(k + 1) * w].bitcast(FP8X4),
-                scales=tsc[:, k * w:(k + 1) * w],
-                in_=grp[hb][:, 4 * k * w:4 * (k + 1) * w],
+                out=tcd[:, k0 * P:k1 * P].bitcast(FP8X4),
+                scales=tsc[:, k0 * P:k1 * P],
+                in_=gpair[hb][:, k0 * 512:k1 * 512],
             )
 
         def passes(hb):
@@ -302,12 +333,9 @@ def tile_waveletlinearlayer_kernel(tc, x, W, b, out):
                     stop=(hb in (ORDER[-1], ORDER[-2]) and ga == 3),
                 )
 
-        prep(0, 2 * X0)
-        for hb in range(1, LEAD):
+        for hb in range(LEAD):
             prep(hb, 1)
-            prep_neg(hb, 0)
-            if hb in XNEGV:
-                prep_neg(hb, 1)
+            neg_v(hb)
         done = 0
         nxt = LEAD
         for hb in range(NHB):
@@ -316,35 +344,29 @@ def tile_waveletlinearlayer_kernel(tc, x, W, b, out):
             if nx < NHB:
                 prep(nx, 1)
                 nxt += 1
-            if hb > 0:
-                for part in t_quant(hb - 1, 1):
-                    part()
+            if hb in TQSEQ:
+                t_quant(TQSEQ[hb] * 4, TQSEQ[hb] * 4 + 8)
             for j in WQSEQ.get(hb, ()):
                 w_quant(2 * j + 1)
-            if nx < NHB and nx not in NEGS:
-                prep_neg(nx, 0)
-            if nx < NHB and nx in XNEGV:
-                prep_neg(nx, 1)
+            if nx < NHB:
+                neg_v(nx)
             if hb == 0:
-                if W0FIRST:
-                    w_front(0)
-                if DB == 0:
-                    raw(0)
-            if DB and (hb + 1) // H == DB:
-                raw(hb + 1)
+                raw(0, 0)
+                raw(0, 1)
+                unit(0, 1)
             unit(hb, 0)
-            if hb == 0 and DB == 0:
-                raw(1)
+            neg_s(hb + NL, 0)
+            if hb == 0:
+                raw(1, 0)
+                raw(1, 1)
             if last:
-                parts = t_quant(hb, 2)
-                parts[0]()
-            unit(hb, 1)
+                t_quant(56, 60)
+                t_quant(60, 62)
+            if hb != 0:
+                unit(hb, 1)
             if last:
-                parts[1]()
-            if hb + NL < NHB:
-                if hb + NL in NEGS:
-                    prep_neg(hb + NL, 0)
-                prep_neg(hb + NL, 1)
+                t_quant(62, 64)
+            neg_s(hb + NL, 1)
             for j in WSEQ[hb]:
                 w_front(j)
             if hb % RUN == 0:
@@ -357,5 +379,7 @@ def tile_waveletlinearlayer_kernel(tc, x, W, b, out):
 
         for h in range(H):
             res = const.tile([P, OUT], F32, name="res%d" % h)
-            nc.vector.tensor_tensor(out=res[:], in0=acc[h][:, 0:OUT], in1=bias_sb[:], op=ADD)
+            nc.vector.scalar_tensor_tensor(
+                out=res[:], in0=acc[h][:, 0:OUT], scalar=0.5, in1=bias_sb[:], op0=MULT, op1=ADD,
+            )
             nc.sync.dma_start(out=out[h * P:(h + 1) * P, :], in_=res[:])

@@ -30,11 +30,12 @@ RUN = 2
 PLAG = 6
 CATCH = {}
 SK = ()
-NAT = ((6, 1), (10, 1), (14, 1))
+NAT = ((6,1),(10,1),(14,1))
 GB = 3
 TB = 5
 TQSEQ = {2: 0, 4: 2, 6: 4, 8: 6, 10: 8, 12: 10, 14: 12}
-HEADX = ((0, 512), (1024, 1536), (512, 1024), (1536, 2048))
+R1 = 0
+DUM = {-1: 1, 1: 1, 2: 1, 3: 1, 4: 1}
 XI = 8
 WQ = 2
 VTAIL = 0
@@ -43,7 +44,7 @@ DG = 1
 WSEQ = ((), (2,), (3,), (4,), (5,), (6,), (7,), (8,), (9,), (10,), (11,), (0, 1), (12, 13), (14,), (15,), ())
 WQSEQ = {4: (1,), 6: (2,), 8: (3,), 10: (4,), 12: (5,), 13: (0,), 14: (6,), 15: (7,)}
 ORDER = (2, 3, 4, 5, 6, 7, 8, 9, 10, 11, 0, 1, 12, 13, 14, 15)
-LOADS = (("x", 2), ("w", 2, 2), ("x", 3), ("x", 4), ("w", 4, 2), ("x", 5), ("x", 6), ("w", 6, 2), ("x", 7), ("x", 8), ("w", 8, 4), ("x", 9), ("x", 10), "d", ("w", 0, 1), ("x", 11), ("w", 12, 4), ("x", 12), ("x", 13), ("x", 14), ("x", 15))
+LOADS = (("x",0,0,512),("x",0,1024,1536),("x",0,512,1024),("x",0,1536,2048),("x",1,0,1024),("x",1,1024,2048), ("x",2),("w",2,2),("x",3),("x",4),("w",4,2),("x",5),("x",6),("w",6,2),("x",7),("x",8),("w",8,4),("x",9),("x",10),"d",("w",0,1),("x",11),("w",12,4),("x",12),("x",13),("x",14),("x",15))
 WDV = 0
 X0 = 2
 WARM = 4
@@ -76,6 +77,10 @@ def tile_waveletlinearlayer_kernel(tc, x, W, b, out):
         warm = xtp.tile([P, 4, P], F32, name="bank")
         for k in range(WARM):
             nc.tensor.matmul(out=warm[:, k % 4, :], lhsT=zero[:], rhs=zero[:], start=True, stop=True)
+
+        def dummy():
+            dt = wtp.tile([P, 4, OUT], F32, name="wT")
+            nc.tensor.matmul(out=dt[:, 0, :], lhsT=zero[:], rhs=zero[:], start=True, stop=True)
 
         identb = const.tile([P, P], BF16, name="identb")
         haar = const.tile([P, 4, 32], BF16, name="haar")
@@ -116,18 +121,14 @@ def tile_waveletlinearlayer_kernel(tc, x, W, b, out):
 
         def load_wd():
             for sub in range(4):
-                c0 = sub * 1024 + DG * 256
+                c0 = DB // 2 * CHW + sub * 1024 + (2 * (DB % 2) + DG) * 256
                 nc.sync.dma_start(out=wd[:, :, sub, :], in_=W[:, c0:c0 + 256].rearrange("p (i j) -> p i j", j=32))
 
-        for c0, c1 in HEADX:
-            load_x(0, c0, c1)
-        load_x(1, 0, 1024)
-        load_x(1, 1024, 2048)
         for item in LOADS:
             if item == "d":
                 load_wd()
             elif item[0] == "x":
-                load_x(item[1], 0, 2048)
+                load_x(item[1], *(item[2:] or (0, 2048)))
             else:
                 load_w(item[1], item[2])
         bias_sb = const.tile([P, OUT], BF16, name="bias_sb")
@@ -149,10 +150,11 @@ def tile_waveletlinearlayer_kernel(tc, x, W, b, out):
             return hb // H == DB and gl == DG
 
         def prep(hb, parts):
+            if hb == 0:
+                parts = 2 * X0
             if hb // H == DB:
-                parts = 2 if hb else 2 * X0
-                if hb not in sd:
-                    prep_parts(hb, parts, range((1 - DG) * parts // 2, (2 - DG) * parts // 2))
+                parts = max(parts, 2)
+                prep_parts(hb, parts, range((1 - DG) * parts // 2, (2 - DG) * parts // 2))
             else:
                 prep_parts(hb, parts, range(parts))
 
@@ -169,6 +171,10 @@ def tile_waveletlinearlayer_kernel(tc, x, W, b, out):
                         in1=xv[:, 1, :, k * ni:(k + 1) * ni, :],
                         op=ADD if sigma == 0 else SUB,
                     )
+                if hb == 0 and DB != 0 and (k + 1) * 2 % parts == 0:
+                    gl = (k + 1) * 2 // parts - 1
+                    if gl < VNEG[0]:
+                        prep_neg(0, gl, gl + 1, True)
 
         def prep_neg(hb, g0, g1, onv):
             n = (g1 - g0) * P
@@ -193,13 +199,11 @@ def tile_waveletlinearlayer_kernel(tc, x, W, b, out):
             for gl in range(2):
                 if (hb, gl) in NAT:
                     natural(hb, gl)
-            if hb < 2:
-                prep_neg(hb, 0, 1, True)
-            elif VNEG[hb]:
+            if VNEG[hb] and (hb or DB == 0):
                 prep_neg(hb, 0, VNEG[hb], True)
 
         def neg_s(hb, gl):
-            if 2 <= hb < NHB and VNEG[hb] <= gl and (hb, gl) not in NAT:
+            if hb < NHB and VNEG[hb] <= gl and (hb, gl) not in NAT and not dense(hb, gl):
                 prep_neg(hb, gl, gl + 1, False)
 
         def w_front(j):
@@ -350,19 +354,29 @@ def tile_waveletlinearlayer_kernel(tc, x, W, b, out):
                 w_quant(2 * j + 1)
             if nx < NHB:
                 neg_v(nx)
-            if hb == 0:
+            if hb == 0 and DB == 0:
                 raw(0, 0)
                 raw(0, 1)
+                for k in range(DUM.get(-1, 0)):
+                    dummy()
                 unit(0, 1)
+            if (hb == 1 and R1 == 1 and DB == 0) or (DB > 0 and hb == 2 * DB + 1):
+                raw(hb, 0)
+                raw(hb, 1)
             unit(hb, 0)
+            for k in range(DUM.get(hb, 0)):
+                dummy()
             neg_s(hb + NL, 0)
             if hb == 0:
-                raw(1, 0)
-                raw(1, 1)
+                for gl in range(2):
+                    neg_s(0, gl)
+            if (hb == 0 and R1 == 0 and DB == 0) or (DB > 0 and hb == 2 * DB - 1):
+                raw(hb + 1, 0)
+                raw(hb + 1, 1)
             if last:
                 t_quant(56, 60)
                 t_quant(60, 62)
-            if hb != 0:
+            if hb or DB != 0:
                 unit(hb, 1)
             if last:
                 t_quant(62, 64)

@@ -24,18 +24,18 @@ FLOPS = 2 * B * OUT * IN
 
 LEAD = 4
 NL = 1
-VNEG = (1, 1, 2, 0, 2, 0, 1, 0, 2, 0, 1, 0, 2, 0, 1, 0)
+VNEG = (1, 1, 2, 0, 2, 0, 2, 0, 2, 0, 2, 0, 2, 0, 1, 0)
 XB = 4
 RUN = 2
 PLAG = 6
 CATCH = {}
 SK = ()
-NAT = ((6,1),(10,1),(14,1))
+NAT = ((14, 1), (15, 1))
 GB = 3
 TB = 5
 TQSEQ = {2: 0, 4: 2, 6: 4, 8: 6, 10: 8, 12: 10, 14: 12}
 R1 = 0
-DUM = {-1: 1, 1: 1, 2: 1, 3: 1, 4: 1}
+DUM = {2: 1, 3: 1, 4: 1, 5: 1, 6: 1}
 XI = 8
 WQ = 2
 VTAIL = 0
@@ -56,7 +56,7 @@ def tile_waveletlinearlayer_kernel(tc, x, W, b, out):
         const = ctx.enter_context(tc.tile_pool(name="const", bufs=1))
         xin = ctx.enter_context(tc.tile_pool(name="xin", bufs=XI))
         win = ctx.enter_context(tc.tile_pool(name="win", bufs=2))
-        sdp = ctx.enter_context(tc.tile_pool(name="sdp", bufs=LEAD + 2))
+        sdp = ctx.enter_context(tc.tile_pool(name="sdp", bufs=6))
         nvp = ctx.enter_context(tc.tile_pool(name="nvp", bufs=4))
         nsp = ctx.enter_context(tc.tile_pool(name="nsp", bufs=NL + 2))
         natp = ctx.enter_context(tc.tile_pool(name="natp", bufs=4))

@@ -34,6 +34,7 @@ NAT = ((14, 1), (15, 1))
 GB = 3
 TB = 5
 TQSEQ = {2: 0, 4: 2, 6: 4, 8: 6, 10: 8, 12: 10, 14: 12}
+IMM = (0, 1, 2, 3)
 R1 = 0
 DUM = {2: 1, 3: 1, 4: 1, 5: 1, 6: 1}
 XI = 8
@@ -149,6 +150,13 @@ def tile_waveletlinearlayer_kernel(tc, x, W, b, out):
         def dense(hb, gl):
             return hb // H == DB and gl == DG
 
+        waiting = []
+
+        def flush():
+            for hb in list(waiting):
+                waiting.remove(hb)
+                neg_v(hb)
+
         def prep(hb, parts):
             if hb == 0:
                 parts = 2 * X0
@@ -171,6 +179,7 @@ def tile_waveletlinearlayer_kernel(tc, x, W, b, out):
                         in1=xv[:, 1, :, k * ni:(k + 1) * ni, :],
                         op=ADD if sigma == 0 else SUB,
                     )
+                    flush()
                 if hb == 0 and DB != 0 and (k + 1) * 2 % parts == 0:
                     gl = (k + 1) * 2 // parts - 1
                     if gl < VNEG[0]:
@@ -339,7 +348,10 @@ def tile_waveletlinearlayer_kernel(tc, x, W, b, out):
 
         for hb in range(LEAD):
             prep(hb, 1)
-            neg_v(hb)
+            if hb in IMM:
+                neg_v(hb)
+            else:
+                waiting.append(hb)
         done = 0
         nxt = LEAD
         for hb in range(NHB):
@@ -348,18 +360,21 @@ def tile_waveletlinearlayer_kernel(tc, x, W, b, out):
             if nx < NHB:
                 prep(nx, 1)
                 nxt += 1
+            if nx < NHB:
+                waiting.append(nx)
             if hb in TQSEQ:
                 t_quant(TQSEQ[hb] * 4, TQSEQ[hb] * 4 + 8)
+                flush()
             for j in WQSEQ.get(hb, ()):
                 w_quant(2 * j + 1)
-            if nx < NHB:
-                neg_v(nx)
+                flush()
             if hb == 0 and DB == 0:
                 raw(0, 0)
                 raw(0, 1)
                 for k in range(DUM.get(-1, 0)):
                     dummy()
                 unit(0, 1)
+                neg_s(0, 0)
             if (hb == 1 and R1 == 1 and DB == 0) or (DB > 0 and hb == 2 * DB + 1):
                 raw(hb, 0)
                 raw(hb, 1)
@@ -367,9 +382,6 @@ def tile_waveletlinearlayer_kernel(tc, x, W, b, out):
             for k in range(DUM.get(hb, 0)):
                 dummy()
             neg_s(hb + NL, 0)
-            if hb == 0:
-                for gl in range(2):
-                    neg_s(0, gl)
             if (hb == 0 and R1 == 0 and DB == 0) or (DB > 0 and hb == 2 * DB - 1):
                 raw(hb + 1, 0)
                 raw(hb + 1, 1)

from contextlib import ExitStack

import concourse.mybir as mybir
from concourse.masks import make_identity

F32 = mybir.dt.float32
BF16 = mybir.dt.bfloat16
U32 = mybir.dt.uint32
U8 = mybir.dt.uint8
FP8X4 = mybir.dt.float8_e4m3fn_x4
ADD = mybir.AluOpType.add
SUB = mybir.AluOpType.subtract
MULT = mybir.AluOpType.mult
COPY = mybir.ActivationFunctionType.Copy

P = 128
B, C, S, OUT = 256, 4, 64, 128
IN = C * S * S
H = B // P
CHW = S * S
NBK = 8
NHB = NBK * H
FLOPS = 2 * B * OUT * IN

LEAD = 4
NL = 1
VNEG = (1, 1, 2, 0, 2, 0, 2, 0, 2, 0, 2, 0, 2, 0, 1, 0)
XB = 4
RUN = 2
PLAG = 6
CATCH = {}
SK = ()
NAT = ((14, 1), (15, 1))
GB = 3
TB = 5
TQSEQ = {2: 0, 4: 2, 6: 4, 8: 6, 10: 8, 12: 10, 14: 12}
IMM = (0, 1, 2, 3)
R1 = 0
DUM = {2: 1, 3: 1, 4: 1, 5: 1, 6: 1}
XI = 8
WQ = 2
VTAIL = 0
DB = 0
DG = 1
WSEQ = ((), (2,), (3,), (4,), (5,), (6,), (7,), (8,), (9,), (10,), (11,), (0, 1), (12, 13), (14,), (15,), ())
WQSEQ = {4: (1,), 6: (2,), 8: (3,), 10: (4,), 12: (5,), 13: (0,), 14: (6,), 15: (7,)}
ORDER = (2, 3, 4, 5, 6, 7, 8, 9, 10, 11, 0, 1, 12, 13, 14, 15)
LOADS = (("x",0,0,512),("x",0,1024,1536),("x",0,512,1024),("x",0,1536,2048),("x",1,0,1024),("x",1,1024,2048), ("x",2),("w",2,2),("x",3),("x",4),("w",4,2),("x",5),("x",6),("w",6,2),("x",7),("x",8),("w",8,4),("x",9),("x",10),"d",("w",0,1),("x",11),("w",12,4),("x",12),("x",13),("x",14),("x",15))
WDV = 0
X0 = 2
WARM = 4


def tile_waveletlinearlayer_kernel(tc, x, W, b, out):
    nc = tc.nc
    with ExitStack() as ctx:
        const = ctx.enter_context(tc.tile_pool(name="const", bufs=1))
        xin = ctx.enter_context(tc.tile_pool(name="xin", bufs=XI))
        win = ctx.enter_context(tc.tile_pool(name="win", bufs=2))
        sdp = ctx.enter_context(tc.tile_pool(name="sdp", bufs=6))
        nvp = ctx.enter_context(tc.tile_pool(name="nvp", bufs=4))
        nsp = ctx.enter_context(tc.tile_pool(name="nsp", bufs=NL + 2))
        natp = ctx.enter_context(tc.tile_pool(name="natp", bufs=4))
        grpp = ctx.enter_context(tc.tile_pool(name="grpp", bufs=GB))
        tqp = ctx.enter_context(tc.tile_pool(name="tqp", bufs=TB))
        wgp = ctx.enter_context(tc.tile_pool(name="wgp", bufs=6 // WQ + 1))
        xtsp = ctx.enter_context(tc.tile_pool(name="xtsp", bufs=4))
        accp = ctx.enter_context(tc.psum_pool(name="accp", bufs=1))
        xtp = ctx.enter_context(tc.psum_pool(name="xtp", bufs=XB))
        wtp = ctx.enter_context(tc.psum_pool(name="wtp", bufs=2))
        ctx.enter_context(tc.manual_schedule())

        ident = const.tile([P, P], F32, name="ident")
        make_identity(nc, ident[:])

        zero = const.tile([P, P], F32, name="zero")
        nc.vector.memset(zero[:], 0.0)
        warm = xtp.tile([P, 4, P], F32, name="bank")
        for k in range(WARM):
            nc.tensor.matmul(out=warm[:, k % 4, :], lhsT=zero[:], rhs=zero[:], start=True, stop=True)

        def dummy():
            dt = wtp.tile([P, 4, OUT], F32, name="wT")
            nc.tensor.matmul(out=dt[:, 0, :], lhsT=zero[:], rhs=zero[:], start=True, stop=True)

        identb = const.tile([P, P], BF16, name="identb")
        haar = const.tile([P, 4, 32], BF16, name="haar")
        half = const.tile([P, 2, 64], F32, name="half")
        nc.vector.tensor_copy(out=identb[:], in_=ident[:])
        cols2 = ident[:].rearrange("p (c e) -> p e c", e=2)
        for c in range(2):
            op = ADD if c == 0 else SUB
            nc.vector.tensor_tensor(out=half[:, c, :], in0=cols2[:, 0, :], in1=cols2[:, 1, :], op=op)
        for c in range(2):
            for r in range(2):
                op = ADD if r == 0 else SUB
                nc.vector.tensor_tensor(out=haar[:, 2 * c + r, :], in0=half[:, c, 0:32], in1=half[:, c, 32:64], op=op)

        wc = const.tile([P, 32 * OUT], U32, name="wc", align_bytes=64)
        ws = const.tile([P, 32 * OUT], U8, name="ws", align_bytes=64)

        x_sb = {}
        w_sb = {}

        def load_x(hb, c0, c1):
            bk, h = hb // H, hb % H
            if hb not in x_sb:
                xt = xin.tile([P, CHW // 2], BF16, name="xt")
                x_sb[hb] = xt
            o = bk * (CHW // 2)
            nc.sync.dma_start(out=x_sb[hb][:, c0:c1], in_=x[h * P:(h + 1) * P, o + c0:o + c1])

        def load_w(j, n):
            ch, g = j // 4, j % 4
            wt = win.tile([P, 4, n * 256], BF16, name="wt%d" % n, bufs=2 if n > 1 else 1)
            for k in range(n):
                w_sb[j + k] = (wt, k * P)
            w4 = W[:, ch * CHW:(ch + 1) * CHW].rearrange("p (s c) -> p s c", s=4)
            nc.sync.dma_start(out=wt[:], in_=w4[:, :, g * 256:(g + n) * 256])

        wd = win.tile([P, 8, 4, 32], BF16, name="wd", bufs=1)

        def load_wd():
            for sub in range(4):
                c0 = DB // 2 * CHW + sub * 1024 + (2 * (DB % 2) + DG) * 256
                nc.sync.dma_start(out=wd[:, :, sub, :], in_=W[:, c0:c0 + 256].rearrange("p (i j) -> p i j", j=32))

        for item in LOADS:
            if item == "d":
                load_wd()
            elif item[0] == "x":
                load_x(item[1], *(item[2:] or (0, 2048)))
            else:
                load_w(item[1], item[2])
        bias_sb = const.tile([P, OUT], BF16, name="bias_sb")
        nc.sync.dma_start(out=bias_sb[:], in_=b.partition_broadcast(P))

        acc0 = accp.tile([P, 512], F32, name="acc0")
        acc1 = accp.tile([P, 512], F32, name="acc1")
        acc = [acc0, acc1]

        sd = {}
        nsd = {}
        grp = {}
        gpair = {}
        tq = {}
        tpair = {}
        wgt = {}

        def dense(hb, gl):
            return hb // H == DB and gl == DG

        waiting = []

        def flush():
            for hb in list(waiting):
                waiting.remove(hb)
                neg_v(hb)

        def prep(hb, parts):
            if hb == 0:
                parts = 2 * X0
            if hb // H == DB:
                parts = max(parts, 2)
                prep_parts(hb, parts, range((1 - DG) * parts // 2, (2 - DG) * parts // 2))
            else:
                prep_parts(hb, parts, range(parts))

        def prep_parts(hb, parts, ks):
            sdt = sdp.tile([P, 2, 4, 256], F32, name="sdt")
            sd[hb] = sdt
            xv = x_sb[hb][:].rearrange("p (i r q v) -> p r v i q", i=16, r=2, q=16, v=4)
            ni = 16 // parts
            for k in ks:
                for sigma in range(2):
                    nc.vector.tensor_tensor(
                        out=sdt[:, sigma, :, k * ni * 16:(k + 1) * ni * 16].rearrange("p v (i q) -> p v i q", q=16),
                        in0=xv[:, 0, :, k * ni:(k + 1) * ni, :],
                        in1=xv[:, 1, :, k * ni:(k + 1) * ni, :],
                        op=ADD if sigma == 0 else SUB,
                    )
                    flush()
                if hb == 0 and DB != 0 and (k + 1) * 2 % parts == 0:
                    gl = (k + 1) * 2 // parts - 1
                    if gl < VNEG[0]:
                        prep_neg(0, gl, gl + 1, True)

        def prep_neg(hb, g0, g1, onv):
            n = (g1 - g0) * P
            nst = (nvp if onv else nsp).tile([P, 2, 2, n], F32, name="nst%d" % n)
            for gl in range(g0, g1):
                nsd[(hb, gl)] = nst[:, :, :, (gl - g0) * P:(gl - g0 + 1) * P]
            odd = sd[hb][:].rearrange("p s (u e) c -> p s u e c", e=2)[:, :, :, 1, g0 * P:g1 * P]
            if onv:
                nc.vector.tensor_scalar_mul(out=nst[:], in0=odd, scalar1=-1.0)
            else:
                nc.scalar.activation(out=nst[:], in_=odd, func=COPY, scale=-1.0)

        nat = {}

        def natural(hb, gl):
            nt = natp.tile([P, 2, P, 2], BF16, name="nt")
            nat[(hb, gl)] = nt
            v = sd[hb][:].rearrange("p s (u e) c -> p s c u e", e=2)[:, :, gl * P:(gl + 1) * P]
            nc.vector.tensor_tensor(out=nt[:], in0=v[:, :, :, :, 0], in1=v[:, :, :, :, 1], op=SUB)

        def neg_v(hb):
            for gl in range(2):
                if (hb, gl) in NAT:
                    natural(hb, gl)
            if VNEG[hb] and (hb or DB == 0):
                prep_neg(hb, 0, VNEG[hb], True)

        def neg_s(hb, gl):
            if hb < NHB and VNEG[hb] <= gl and (hb, gl) not in NAT and not dense(hb, gl):
                prep_neg(hb, gl, gl + 1, False)

        def w_front(j):
            bk, gl = j // 2, j % 2
            ch, g = bk // 2, 2 * (bk % 2) + gl
            if j - j % WQ not in wgt:
                wg = wgp.tile([P, WQ * 1024], BF16, name="wg", align_bytes=64)
                wgt[j - j % WQ] = wg
            wg = wgt[j - j % WQ]
            h0 = (j % WQ) * 1024
            if dense(2 * bk, gl):
                wTb = wtp.tile([P, 8, OUT], BF16, name="wT")
                for i in range(8):
                    nc.tensor.transpose(wTb[:, i, :], wd[:, i, :, :].rearrange("p s j -> p (s j)"), identb[:])
                (nc.vector.tensor_copy if WDV else nc.scalar.copy)(
                    out=wg[:, h0:h0 + 1024].rearrange("p (a o t) -> p a o t", a=2, o=OUT, t=4),
                    in_=wTb[:].rearrange("p (a t) o -> p a o t", a=2, t=4),
                )
                return
            wt, wo = w_sb[j]
            wT = wtp.tile([P, 4, OUT], F32, name="wT")
            for sub in range(4):
                nc.tensor.transpose(wT[:, sub, :], wt[:, sub, :].bitcast(F32)[:, wo:wo + P], ident[:])
            nc.scalar.copy(
                out=wg[:, h0:h0 + 1024].bitcast(F32).rearrange("p (a o s) -> p a o s", a=2, o=OUT, s=2),
                in_=wT[:].rearrange("p (a s) o -> p a o s", a=2, s=2),
            )

        def w_quant(j):
            if (j + 1) % WQ:
                return
            j0 = j + 1 - WQ
            c0, c1 = j0 * 256, (j + 1) * 256
            nc.vector.quantize_mx(out=wc[:, c0:c1].bitcast(FP8X4), scales=ws[:, c0:c1], in_=wgt[j0][:])

        xts = {}

        def raw(hb, a):
            bankr = xtp.tile([P, 4, P], BF16, name="bank")
            for i in range(4):
                c0 = DG * 1024 + (4 * a + i) * P
                nc.tensor.transpose(bankr[:, i, :], x_sb[hb][:, c0:c0 + P], identb[:])
            xt = xtsp.tile([P, 4, P], BF16, name="xT")
            xts[(hb, a)] = xt
            nc.scalar.copy(out=xt[:], in_=bankr[:])

        def unit(hb, gl):
            if hb not in grp:
                gt = grpp.tile([P, 4096], BF16, name="gt", align_bytes=64)
                grp[hb] = gt[:, 0:2048]
                grp[hb + 1] = gt[:, 2048:4096]
                gpair[hb] = gt
            if dense(hb, gl):
                for a in range(2):
                    bank = xtp.tile([P, 4, P], F32, name="bank")
                    nc.tensor.matmul(
                        out=bank[:].rearrange("p k n -> p (k n)"), lhsT=haar[:].rearrange("p s j -> p (s j)"),
                        rhs=xts[(hb, a)][:].rearrange("p k n -> p (k n)"), start=True, stop=True,
                    )
                    c0 = (gl * 2 + a) * 512
                    nc.scalar.activation(
                        out=grp[hb][:, c0:c0 + 512].rearrange("p (n k) -> p n k", k=4),
                        in_=bank[:].rearrange("p k n -> p n k"), func=COPY, scale=1.0,
                    )
                return
            cols = slice(gl * P, (gl + 1) * P)
            s = sd[hb]
            for a in range(2):
                bank = xtp.tile([P, 4, P], F32, name="bank")
                if a == 1 and (hb, gl) in nat:
                    nt = nat[(hb, gl)][:].rearrange("p s c u -> p s (c u)")
                    for sigma in range(2):
                        nc.tensor.transpose(bank[:, sigma, :], nt[:, sigma, :].bitcast(F32), ident[:])
                    c0 = (gl * 2 + a) * 512
                    nc.scalar.copy(
                        out=grp[hb][:, c0:c0 + 512].bitcast(F32).rearrange("p (n k) -> p n k", k=2),
                        in_=bank[:, 0:2, :].rearrange("p k n -> p n k"),
                    )
                    continue
                for sigma in range(2):
                    for u in range(2):
                        second = s[:, sigma, 2 * u + 1, cols] if a == 0 else nsd[(hb, gl)][:, sigma, u, :]
                        nc.tensor.matmul(
                            out=bank[:, 2 * sigma + u, :], lhsT=s[:, sigma, 2 * u, cols], rhs=ident[:],
                            start=True, stop=False, is_transpose=True,
                        )
                        nc.tensor.matmul(
                            out=bank[:, 2 * sigma + u, :], lhsT=second, rhs=ident[:],
                            start=False, stop=True, is_transpose=True,
                        )
                c0 = (gl * 2 + a) * 512
                if hb == NHB - 1 and gl * 2 + a >= 4 - VTAIL:
                    nc.vector.tensor_scalar_mul(
                        out=grp[hb][:, c0:c0 + 512].rearrange("p (n k) -> p n k", k=4),
                        in0=bank[:].rearrange("p k n -> p n k"), scalar1=1.0,
                    )
                    continue
                nc.scalar.activation(
                    out=grp[hb][:, c0:c0 + 512].rearrange("p (n k) -> p n k", k=4),
                    in_=bank[:].rearrange("p k n -> p n k"), func=COPY, scale=1.0,
                )

        def t_quant(b0, b1):
            hb = b0 // 8 * 2
            if hb not in tq:
                tcd = tqp.tile([P, 1024], U32, name="tcd", align_bytes=64)
                tsc = tqp.tile([P, 1024], U8, name="tsc", align_bytes=64)
                tq[hb] = (tcd[:, 0:512], tsc[:, 0:512])
                tq[hb + 1] = (tcd[:, 512:1024], tsc[:, 512:1024])
                tpair[hb] = (tcd, tsc)
            tcd, tsc = tpair[hb]
            k0, k1 = b0 - 4 * hb, b1 - 4 * hb
            nc.vector.quantize_mx(
                out=tcd[:, k0 * P:k1 * P].bitcast(FP8X4),
                scales=tsc[:, k0 * P:k1 * P],
                in_=gpair[hb][:, k0 * 512:k1 * 512],
            )

        def passes(hb):
            bk, h = hb // H, hb % H
            tcd, tsc = tq[hb]
            for ga in range(4):
                w0 = (bk * 4 + ga) * OUT
                nc.tensor.matmul_mx(
                    out=acc[h][:, 0:OUT],
                    lhsT=tcd[:, ga * P:(ga + 1) * P].bitcast(FP8X4),
                    lhsT_scale=tsc[:, ga * P:(ga + 1) * P],
                    rhs=wc[:, w0:w0 + OUT].bitcast(FP8X4),
                    rhs_scale=ws[:, w0:w0 + OUT],
                    start=(hb in (ORDER[0], ORDER[1]) and ga == 0),
                    stop=(hb in (ORDER[-1], ORDER[-2]) and ga == 3),
                )

        for hb in range(LEAD):
            prep(hb, 1)
            if hb in IMM:
                neg_v(hb)
            else:
                waiting.append(hb)
        done = 0
        nxt = LEAD
        for hb in range(NHB):
            last = hb == NHB - 1
            nx = nxt if hb not in SK else NHB
            if nx < NHB:
                prep(nx, 1)
                nxt += 1
            if nx < NHB:
                waiting.append(nx)
            if hb in TQSEQ:
                t_quant(TQSEQ[hb] * 4, TQSEQ[hb] * 4 + 8)
                flush()
            for j in WQSEQ.get(hb, ()):
                w_quant(2 * j + 1)
                flush()
            if hb == 0 and DB == 0:
                raw(0, 0)
                raw(0, 1)
                for k in range(DUM.get(-1, 0)):
                    dummy()
                unit(0, 1)
                neg_s(0, 0)
            if (hb == 1 and R1 == 1 and DB == 0) or (DB > 0 and hb == 2 * DB + 1):
                raw(hb, 0)
                raw(hb, 1)
            unit(hb, 0)
            for k in range(DUM.get(hb, 0)):
                dummy()
            neg_s(hb + NL, 0)
            if (hb == 0 and R1 == 0 and DB == 0) or (DB > 0 and hb == 2 * DB - 1):
                raw(hb + 1, 0)
                raw(hb + 1, 1)
            if last:
                t_quant(56, 60)
                t_quant(60, 62)
            if hb or DB != 0:
                unit(hb, 1)
            if last:
                t_quant(62, 64)
            neg_s(hb + NL, 1)
            for j in WSEQ[hb]:
                w_front(j)
            if hb % RUN == 0:
                while done < CATCH.get(hb, hb - PLAG):
                    passes(ORDER[done])
                    done += 1
        while done < NHB:
            passes(ORDER[done])
            done += 1

        for h in range(H):
            res = const.tile([P, OUT], F32, name="res%d" % h)
            nc.vector.scalar_tensor_tensor(
                out=res[:], in0=acc[h][:, 0:OUT], scalar=0.5, in1=bias_sb[:], op0=MULT, op1=ADD,
            )
            nc.sync.dma_start(out=out[h * P:(h + 1) * P, :], in_=res[:])
